import numpy as np
import ml_dtypes


def mxq(x, axis, fmt="e4m3"):
    dtype, down = {"e4m3": (ml_dtypes.float8_e4m3fn, 7), "e5m2": (ml_dtypes.float8_e5m2, 14)}[fmt]
    v = np.moveaxis(np.asarray(x, np.float32).astype(ml_dtypes.bfloat16).astype(np.float64), axis, -1)
    blocks = v.reshape(v.shape[:-1] + (-1, 32))
    amax = np.abs(blocks).max(-1, keepdims=True)
    byte = np.maximum(np.where(amax > 0, np.frexp(amax)[1] - 1 + 127, 0) - down, 1)
    scale = np.exp2(byte - 127.0)
    codes = (blocks / scale).astype(np.float32).astype(dtype).astype(np.float64)
    return np.moveaxis((codes * scale).reshape(v.shape), -1, axis)


WIDE = False


def mx_kscale(k):
    if not WIDE:
        return np.ones(k)
    levels = np.array([10, -10, 5, -5, 0])
    a = np.random.permutation(np.resize(levels, k // 512 * 4)).reshape(k // 512, 4)
    idx = np.arange(k)
    return np.exp2(a[idx // 512, idx % 128 // 32])


BF16 = ml_dtypes.bfloat16


def bf(x):
    return np.asarray(x, np.float32).astype(BF16)


def f64(x):
    return np.asarray(x).astype(np.float64)


B, N, IN, H, D = 2, 64, 512, 8, 64
LN_EPS = 1e-5


def layer_norm(x, g, b):
    m = x.mean(-1, keepdims=True)
    v = ((x - m) ** 2).mean(-1, keepdims=True)
    return (x - m) / np.sqrt(v + LN_EPS) * g + b


def setup_inputs():
    t = mx_kscale(IN)
    u = np.concatenate([t, t, np.ones(IN)])
    keep = np.random.random((B, N)) < 0.9
    return {"new_node": bf(np.random.standard_normal((B, N, IN)) * t),
            "emb_edge": bf(np.random.standard_normal((B, N, N, IN))),
            "node_mask": bf(keep * (0.5 + 0.5 * np.random.random((B, N)))),
            "Wedge": bf(np.random.standard_normal((3 * IN, IN)) / np.sqrt(IN) / u[:, None]),
            "bedge": bf(np.random.standard_normal(IN) * 0.3),
            "gamma_e": bf(1.0 + 0.1 * np.random.standard_normal(IN)),
            "beta_e": bf(0.1 * np.random.standard_normal(IN))}


def reference(new_node, emb_edge, node_mask, Wedge, bedge, gamma_e, beta_e):
    x_mask = f64(node_mask)[..., None]
    e_mask = x_mask[:, :, None, :] * x_mask[:, None, :, :]
    xe = f64(emb_edge) * e_mask
    wq = mxq(f64(Wedge), 0, "e4m3")
    nq = mxq(f64(new_node), 2, "e4m3")
    p_row = nq @ wq[:IN]
    p_col = nq @ wq[IN:IN + IN]
    p_edge = mxq(xe, 3, "e4m3") @ wq[IN + IN:]
    new_edge = p_row[:, :, None] + p_col[:, None] + p_edge + f64(bedge)
    return layer_norm(xe + new_edge, f64(gamma_e), f64(beta_e))

@@ -1,0 +1,266 @@
+import concourse.mybir as mybir
+from concourse.masks import make_identity
+
+BF16 = mybir.dt.bfloat16
+F32 = mybir.dt.float32
+I32 = mybir.dt.int32
+U32 = mybir.dt.uint32
+U8 = mybir.dt.uint8
+FP8X4 = mybir.dt.float8_e4m3fn_x4
+ALU = mybir.AluOpType
+ACT = mybir.ActivationFunctionType
+
+P = 128
+PACK = 4
+GRAPHS = 2
+NODES = 64
+FEAT = 512
+GROUP = 4
+PAIR = 2
+REP = 4
+LN_EPS = 1e-5
+
+FLOPS = 2 * (GRAPHS * NODES * NODES + 2 * GRAPHS * NODES) * FEAT * FEAT
+
+
+def tile_densegatlayer_pb_kernel(
+    tc, new_node, emb_edge, node_mask, Wedge, bedge, gamma_e, beta_e, out
+):
+    nc = tc.nc
+    emb_rows = emb_edge.rearrange("b i j f -> (b i) j f")
+    out_rows = out.rearrange("b i j f -> (b i) j f")
+
+    with (
+        tc.tile_pool(name="consts", bufs=1) as consts,
+        tc.tile_pool(name="w_stage", bufs=3) as w_stage,
+        tc.tile_pool(name="emb_pool", bufs=6) as emb_pool,
+        tc.tile_pool(name="front", bufs=3) as front,
+        tc.tile_pool(name="back", bufs=3) as back,
+        tc.tile_pool(name="small", bufs=4) as small,
+        tc.psum_pool(name="psum_const", bufs=1) as psum_const,
+        tc.psum_pool(name="psum_t", bufs=2) as psum_t,
+        tc.psum_pool(name="psum_acc", bufs=4) as psum_acc,
+    ):
+        mask_col_bf = consts.tile([P, 1], BF16, name="mask_col_bf")
+        nc.scalar.dma_start(out=mask_col_bf[:], in_=node_mask.rearrange("b (n o) -> (b n) o", o=1))
+        mask_row = consts.tile([P, NODES], BF16, name="mask_row")
+        for b in range(GRAPHS):
+            nc.scalar.dma_start(
+                out=mask_row[b * NODES : (b + 1) * NODES, :],
+                in_=node_mask[b : b + 1, :].rearrange("o n -> (o n)").partition_broadcast(NODES),
+            )
+        node_sb = consts.tile([P, FEAT], BF16, name="node_sb")
+        nc.scalar.dma_start(out=node_sb[:], in_=new_node.rearrange("b n f -> (b n) f"))
+        vec_rows = consts.tile([P, 3, FEAT], BF16, name="vec_rows")
+        nc.vector.memset(vec_rows[:], 0.0)
+        for v, vec in enumerate((gamma_e, beta_e, bedge)):
+            nc.scalar.dma_start(out=vec_rows[0:1, v, :], in_=vec.rearrange("(o f) -> o f", o=1))
+
+        ident = consts.tile([P, P], BF16, name="ident")
+        make_identity(nc, ident[:])
+        ones = consts.tile([P, P], BF16, name="ones")
+        nc.vector.memset(ones[:], 1.0)
+        eps = consts.tile([P, 1], F32, name="eps")
+        nc.vector.memset(eps[:], LN_EPS)
+
+        mask_col = consts.tile([P, 1], F32, name="mask_col")
+        nc.vector.tensor_copy(out=mask_col[:], in_=mask_col_bf[:])
+        e_mask = consts.tile([P, NODES], F32, name="e_mask")
+        nc.vector.tensor_scalar_mul(out=e_mask[:], in0=mask_row[:], scalar1=mask_col[:, 0:1])
+
+        w_codes = consts.tile([P, 3, FEAT], U32, name="w_codes", align_bytes=64)
+        w_scales = consts.tile([P, 3, FEAT], U8, name="w_scales", align_bytes=64)
+        w_grouped = []
+        for blk in (2, 1, 0):
+            w_raw = w_stage.tile([P, PACK, FEAT], BF16, name="w_raw")
+            nc.sync.dma_start(
+                out=w_raw[:],
+                in_=Wedge[blk * FEAT : (blk + 1) * FEAT, :].rearrange("(t p) n -> p t n", p=P),
+            )
+            grouped_w = w_stage.tile([P, FEAT, PACK], BF16, name="grouped_w", align_bytes=64)
+            nc.vector.tensor_copy(out=grouped_w[:], in_=w_raw[:].rearrange("p t n -> p n t"))
+            w_grouped.append((blk, grouped_w))
+        for blk, grouped_w in w_grouped:
+            nc.vector.quantize_mx(
+                out=w_codes[:, blk, :].bitcast(FP8X4),
+                scales=w_scales[:, blk, :],
+                in_=grouped_w[:].rearrange("p n t -> p (n t)"),
+            )
+
+        gamma_ps = psum_const.tile([P, FEAT], F32, name="gamma_ps")
+        nc.tensor.matmul(out=gamma_ps[:], lhsT=ones[:], rhs=vec_rows[:, 0, :], start=True, stop=True)
+        beta_ps = psum_const.tile([P, FEAT], F32, name="beta_ps")
+        nc.tensor.matmul(out=beta_ps[:], lhsT=ones[:], rhs=vec_rows[:, 1, :], start=True, stop=True)
+        bias_ps = psum_acc.tile([P, FEAT], F32, name="acc")
+        nc.tensor.matmul(out=bias_ps[:], lhsT=ones[:], rhs=vec_rows[:, 2, :], start=True, stop=True)
+        bias_all = consts.tile([P, FEAT], F32, name="bias_all")
+        nc.vector.tensor_copy(out=bias_all[:], in_=bias_ps[:])
+
+        node_t = psum_t.tile([P, PAIR, PACK, P], BF16, name="xt")
+        for t in range(PACK):
+            nc.tensor.transpose(node_t[:, 0, t, :], node_sb[:, t * P : (t + 1) * P], ident[:])
+        node_grouped = consts.tile([P, P, PACK], BF16, name="node_grouped", align_bytes=64)
+        nc.vector.tensor_copy(out=node_grouped[:], in_=node_t[:, 0, :, :].rearrange("p t n -> p n t"))
+        col_grouped = consts.tile([P, NODES, GRAPHS, REP, PACK], BF16, name="col_grouped", align_bytes=64)
+        for b in range(GRAPHS):
+            nc.vector.tensor_copy(
+                out=col_grouped[:, :, b, :, :],
+                in_=node_t[:, 0, :, b * NODES : (b + 1) * NODES]
+                .rearrange("p t j -> p j t")
+                .unsqueeze(2)
+                .to_broadcast([P, NODES, REP, PACK]),
+            )
+        node_codes = consts.tile([P, P], U32, name="node_codes", align_bytes=64)
+        node_scales = consts.tile([P, P], U8, name="node_scales", align_bytes=64)
+        nc.vector.quantize_mx(
+            out=node_codes[:].bitcast(FP8X4),
+            scales=node_scales[:],
+            in_=node_grouped[:].rearrange("p n t -> p (n t)"),
+        )
+        col4_codes = consts.tile([P, NODES * GRAPHS, REP], U32, name="col4_codes", align_bytes=64)
+        col4_scales = consts.tile([P, NODES * GRAPHS, REP], U8, name="col4_scales", align_bytes=64)
+        nc.vector.memset(col4_scales[:].bitcast(I32), 0)
+        nc.vector.quantize_mx(
+            out=col4_codes[:].rearrange("p a r -> p (a r)").bitcast(FP8X4),
+            scales=col4_scales[:].rearrange("p a r -> p (a r)"),
+            in_=col_grouped[:].rearrange("p j b r t -> p (j b r t)"),
+        )
+        col_codes = consts.tile([P, NODES, P], U32, name="col_codes", align_bytes=64)
+        col_scales = consts.tile([P, NODES, P], U8, name="col_scales", align_bytes=64)
+        nc.vector.tensor_copy(
+            out=col_scales[:].bitcast(I32).rearrange("p j (b s) -> p (j b) s", b=GRAPHS),
+            in_=col4_scales[:].bitcast(I32).to_broadcast([P, NODES * GRAPHS, NODES // REP]),
+        )
+        for q in range(4):
+            js = slice(q * NODES // 4, (q + 1) * NODES // 4)
+            ab = slice(q * NODES * GRAPHS // 4, (q + 1) * NODES * GRAPHS // 4)
+            nc.vector.tensor_copy(
+                out=col_codes[:, js, :].bitcast(I32).rearrange("p j (b s r) -> p (j b) s r", b=GRAPHS, r=REP),
+                in_=col4_codes[:, ab, :]
+                .bitcast(I32)
+                .unsqueeze(2)
+                .to_broadcast([P, NODES * GRAPHS // 4, NODES // REP, REP]),
+            )
+
+        row_ps = psum_acc.tile([P, FEAT], F32, name="acc")
+        nc.tensor.matmul_mx(
+            out=row_ps[:],
+            lhsT=node_codes[:].bitcast(FP8X4),
+            lhsT_scale=node_scales[:],
+            rhs=w_codes[:, 0, :].bitcast(FP8X4),
+            rhs_scale=w_scales[:, 0, :],
+            start=True,
+            stop=True,
+        )
+        c = consts.tile([P, FEAT], F32, name="c")
+        c_sum = consts.tile([P, 1], F32, name="c_sum")
+        nc.vector.scalar_tensor_tensor(
+            out=c[:], in0=row_ps[:], scalar=1.0, in1=bias_all[:], op0=ALU.mult, op1=ALU.add, accum_out=c_sum[:]
+        )
+
+        for g in range(NODES // GROUP):
+            j0 = g * GROUP
+            emb_sb = emb_pool.tile([P, GROUP, FEAT], BF16, name="emb_sb")
+            nc.sync.dma_start(out=emb_sb[:], in_=emb_rows[:, j0 : j0 + GROUP, :])
+
+            xe_bf = front.tile([P, GROUP, FEAT], BF16, name="xe_bf")
+            for k in range(GROUP):
+                nc.scalar.activation(
+                    out=xe_bf[:, k, :], in_=emb_sb[:, k, :], func=ACT.Copy, scale=e_mask[:, j0 + k : j0 + k + 1]
+                )
+            grouped = front.tile([P, GROUP, P, PACK], BF16, name="grouped", align_bytes=64)
+            for h in range(GROUP // PAIR):
+                xt = psum_t.tile([P, PAIR, PACK, P], BF16, name="xt")
+                for k in range(PAIR):
+                    for t in range(PACK):
+                        nc.tensor.transpose(xt[:, k, t, :], xe_bf[:, h * PAIR + k, t * P : (t + 1) * P], ident[:])
+                nc.scalar.copy(
+                    out=grouped[:, h * PAIR : (h + 1) * PAIR, :, :], in_=xt[:].rearrange("p k t r -> p k r t")
+                )
+            codes = front.tile([P, GROUP, P], U32, name="codes", align_bytes=64)
+            scales = front.tile([P, GROUP, P], U8, name="scales", align_bytes=64)
+            nc.vector.quantize_mx(
+                out=codes[:].rearrange("p k r -> p (k r)").bitcast(FP8X4),
+                scales=scales[:].rearrange("p k r -> p (k r)"),
+                in_=grouped[:].rearrange("p k r t -> p (k r t)"),
+            )
+
+            y = back.tile([P, GROUP, FEAT], F32, name="y")
+            row_sum = small.tile([P, GROUP], F32, name="row_sum")
+            for k in range(GROUP):
+                j = j0 + k
+                acc = psum_acc.tile([P, FEAT], F32, name="acc")
+                nc.tensor.matmul_mx(
+                    out=acc[:],
+                    lhsT=codes[:, k, :].bitcast(FP8X4),
+                    lhsT_scale=scales[:, k, :],
+                    rhs=w_codes[:, 2, :].bitcast(FP8X4),
+                    rhs_scale=w_scales[:, 2, :],
+                    start=True,
+                    stop=False,
+                )
+                nc.tensor.matmul_mx(
+                    out=acc[:],
+                    lhsT=col_codes[:, j, :].bitcast(FP8X4),
+                    lhsT_scale=col_scales[:, j, :],
+                    rhs=w_codes[:, 1, :].bitcast(FP8X4),
+                    rhs_scale=w_scales[:, 1, :],
+                    start=False,
+                    stop=True,
+                )
+                nc.vector.scalar_tensor_tensor(
+                    out=y[:, k, :],
+                    in0=emb_sb[:, k, :],
+                    scalar=e_mask[:, j : j + 1],
+                    in1=acc[:],
+                    op0=ALU.mult,
+                    op1=ALU.add,
+                    accum_out=row_sum[:, k : k + 1],
+                )
+                nc.gpsimd.tensor_tensor(out=y[:, k, :], in0=y[:, k, :], in1=c[:], op=ALU.add)
+
+            neg_mean = small.tile([P, GROUP], F32, name="neg_mean")
+            nc.vector.tensor_scalar(
+                out=neg_mean[:],
+                in0=row_sum[:],
+                scalar1=c_sum[:, 0:1],
+                scalar2=-1.0 / FEAT,
+                op0=ALU.add,
+                op1=ALU.mult,
+            )
+            sq_sum = small.tile([P, GROUP], F32, name="sq_sum")
+            for k in range(GROUP):
+                squares = small.tile([P, FEAT], BF16, name="squares")
+                nc.scalar.activation(
+                    out=squares[:],
+                    in_=y[:, k, :],
+                    func=ACT.Square,
+                    bias=neg_mean[:, k : k + 1],
+                    scale=1.0,
+                    accum_out=sq_sum[:, k : k + 1],
+                )
+            std = small.tile([P, GROUP], F32, name="std")
+            nc.scalar.activation(out=std[:], in_=sq_sum[:], func=ACT.Sqrt, bias=eps[:, 0:1], scale=1.0 / FEAT)
+            rstd = small.tile([P, GROUP], F32, name="rstd")
+            nc.vector.reciprocal(out=rstd[:], in_=std[:])
+
+            res = back.tile([P, GROUP, FEAT], F32, name="res")
+            for k in range(GROUP):
+                nc.vector.scalar_tensor_tensor(
+                    out=res[:, k, :],
+                    in0=y[:, k, :],
+                    scalar=neg_mean[:, k : k + 1],
+                    in1=gamma_ps[:],
+                    op0=ALU.add,
+                    op1=ALU.mult,
+                )
+            for k in range(GROUP):
+                nc.vector.scalar_tensor_tensor(
+                    out=res[:, k, :],
+                    in0=res[:, k, :],
+                    scalar=rstd[:, k : k + 1],
+                    in1=beta_ps[:],
+                    op0=ALU.mult,
+                    op1=ALU.add,
+                )
+            nc.sync.dma_start(out=out_rows[:, j0 : j0 + GROUP, :], in_=res[:])

@@ -16,8 +16,10 @@ GRAPHS = 2
 NODES = 64
 FEAT = 512
 GROUP = 4
+N_GROUPS = NODES // GROUP
 PAIR = 2
 REP = 4
+LOADS_AHEAD = 4
 LN_EPS = 1e-5
 
 FLOPS = 2 * (GRAPHS * NODES * NODES + 2 * GRAPHS * NODES) * FEAT * FEAT
@@ -33,14 +35,22 @@ def tile_densegatlayer_pb_kernel(
     with (
         tc.tile_pool(name="consts", bufs=1) as consts,
         tc.tile_pool(name="w_stage", bufs=3) as w_stage,
-        tc.tile_pool(name="emb_pool", bufs=6) as emb_pool,
-        tc.tile_pool(name="front", bufs=3) as front,
+        tc.tile_pool(name="emb_pool", bufs=LOADS_AHEAD + 2) as emb_pool,
+        tc.tile_pool(name="front", bufs=2) as front,
         tc.tile_pool(name="back", bufs=3) as back,
         tc.tile_pool(name="small", bufs=4) as small,
         tc.psum_pool(name="psum_const", bufs=1) as psum_const,
         tc.psum_pool(name="psum_t", bufs=2) as psum_t,
-        tc.psum_pool(name="psum_acc", bufs=4) as psum_acc,
+        tc.psum_pool(name="psum_acc", bufs=GROUP) as psum_acc,
+        tc.manual_schedule(),
     ):
+        emb_sb, grouped, codes, scales, col_codes, col_scales = {}, {}, {}, {}, {}, {}
+        acc, y, row_sum, neg_mean, std, res = {}, {}, {}, {}, {}, {}
+
+        def load(g):
+            emb_sb[g] = emb_pool.tile([P, GROUP, FEAT], BF16, name="emb_sb")
+            nc.sync.dma_start(out=emb_sb[g][:], in_=emb_rows[:, g * GROUP : (g + 1) * GROUP, :])
+
         mask_col_bf = consts.tile([P, 1], BF16, name="mask_col_bf")
         nc.scalar.dma_start(out=mask_col_bf[:], in_=node_mask.rearrange("b (n o) -> (b n) o", o=1))
         mask_row = consts.tile([P, NODES], BF16, name="mask_row")
@@ -51,41 +61,222 @@ def tile_densegatlayer_pb_kernel(
             )
         node_sb = consts.tile([P, FEAT], BF16, name="node_sb")
         nc.scalar.dma_start(out=node_sb[:], in_=new_node.rearrange("b n f -> (b n) f"))
-        vec_rows = consts.tile([P, 3, FEAT], BF16, name="vec_rows")
-        nc.vector.memset(vec_rows[:], 0.0)
-        for v, vec in enumerate((gamma_e, beta_e, bedge)):
-            nc.scalar.dma_start(out=vec_rows[0:1, v, :], in_=vec.rearrange("(o f) -> o f", o=1))
+        load(0)
+        w_raw = {}
+        for blk in (2, 1, 0):
+            w_raw[blk] = w_stage.tile([P, PACK, FEAT], BF16, name="w_raw")
+            nc.sync.dma_start(
+                out=w_raw[blk][:],
+                in_=Wedge[blk * FEAT : (blk + 1) * FEAT, :].rearrange("(t p) n -> p t n", p=P),
+            )
+        for g in range(1, LOADS_AHEAD):
+            load(g)
 
         ident = consts.tile([P, P], BF16, name="ident")
         make_identity(nc, ident[:])
+        vec_rows = consts.tile([P, 3, FEAT], BF16, name="vec_rows")
+        nc.vector.memset(vec_rows[:], 0.0)
+        for v, vec in enumerate((gamma_e, beta_e, bedge)):
+            nc.gpsimd.dma_start(out=vec_rows[0:1, v, :], in_=vec.rearrange("(o f) -> o f", o=1))
         ones = consts.tile([P, P], BF16, name="ones")
         nc.vector.memset(ones[:], 1.0)
         eps = consts.tile([P, 1], F32, name="eps")
         nc.vector.memset(eps[:], LN_EPS)
+        warm = consts.tile([P, 1], F32, name="warm")
+        nc.scalar.activation(out=warm[:], in_=eps[:], func=ACT.Sqrt)
 
         mask_col = consts.tile([P, 1], F32, name="mask_col")
         nc.vector.tensor_copy(out=mask_col[:], in_=mask_col_bf[:])
         e_mask = consts.tile([P, NODES], F32, name="e_mask")
         nc.vector.tensor_scalar_mul(out=e_mask[:], in0=mask_row[:], scalar1=mask_col[:, 0:1])
 
+        def mask_and_transpose(g):
+            xe_bf = front.tile([P, GROUP, FEAT], BF16, name="xe_bf")
+            for k in range(GROUP):
+                j = g * GROUP + k
+                nc.scalar.activation(
+                    out=xe_bf[:, k, :], in_=emb_sb[g][:, k, :], func=ACT.Copy, scale=e_mask[:, j : j + 1]
+                )
+            grouped[g] = front.tile([P, GROUP, P, PACK], BF16, name="grouped", align_bytes=64)
+            for h in range(GROUP // PAIR):
+                xt = psum_t.tile([P, PAIR, PACK, P], BF16, name="xt")
+                for k in range(PAIR):
+                    for t in range(PACK):
+                        nc.tensor.transpose(xt[:, k, t, :], xe_bf[:, h * PAIR + k, t * P : (t + 1) * P], ident[:])
+                nc.scalar.copy(
+                    out=grouped[g][:, h * PAIR : (h + 1) * PAIR, :, :], in_=xt[:].rearrange("p k t r -> p k r t")
+                )
+
+        def quantise(g):
+            codes[g] = front.tile([P, GROUP, P], U32, name="codes", align_bytes=64)
+            scales[g] = front.tile([P, GROUP, P], U8, name="scales", align_bytes=64)
+            nc.vector.quantize_mx(
+                out=codes[g][:].rearrange("p k r -> p (k r)").bitcast(FP8X4),
+                scales=scales[g][:].rearrange("p k r -> p (k r)"),
+                in_=grouped[g][:].rearrange("p k r t -> p (k r t)"),
+            )
+            col_codes[g] = front.tile([P, GROUP, P], U32, name="col_codes", align_bytes=64)
+            col_scales[g] = front.tile([P, GROUP, P], U8, name="col_scales", align_bytes=64)
+            pairs = slice(g * GROUP * GRAPHS, (g + 1) * GROUP * GRAPHS)
+            nc.vector.tensor_copy(
+                out=col_codes[g][:].bitcast(I32).rearrange("p k (b s r) -> p (k b) s r", b=GRAPHS, r=REP),
+                in_=col4_codes[:, pairs, :]
+                .bitcast(I32)
+                .unsqueeze(2)
+                .to_broadcast([P, GROUP * GRAPHS, NODES // REP, REP]),
+            )
+            nc.vector.tensor_copy(
+                out=col_scales[g][:].bitcast(I32).rearrange("p k (b s) -> p (k b) s", b=GRAPHS),
+                in_=col4_scales[:, pairs, :].bitcast(I32).to_broadcast([P, GROUP * GRAPHS, NODES // REP]),
+            )
+
+        def products(g):
+            acc[g] = []
+            for k in range(GROUP):
+                bank = psum_acc.tile([P, FEAT], F32, name="acc")
+                nc.tensor.matmul_mx(
+                    out=bank[:],
+                    lhsT=codes[g][:, k, :].bitcast(FP8X4),
+                    lhsT_scale=scales[g][:, k, :],
+                    rhs=w_codes[:, 2, :].bitcast(FP8X4),
+                    rhs_scale=w_scales[:, 2, :],
+                    start=True,
+                    stop=False,
+                )
+                nc.tensor.matmul_mx(
+                    out=bank[:],
+                    lhsT=col_codes[g][:, k, :].bitcast(FP8X4),
+                    lhsT_scale=col_scales[g][:, k, :],
+                    rhs=w_codes[:, 1, :].bitcast(FP8X4),
+                    rhs_scale=w_scales[:, 1, :],
+                    start=False,
+                    stop=True,
+                )
+                acc[g].append(bank)
+
+        def residual(g):
+            y[g] = back.tile([P, GROUP, FEAT], F32, name="y")
+            row_sum[g] = small.tile([P, GROUP], F32, name="row_sum")
+            for k in range(GROUP):
+                j = g * GROUP + k
+                nc.vector.scalar_tensor_tensor(
+                    out=y[g][:, k, :],
+                    in0=emb_sb[g][:, k, :],
+                    scalar=e_mask[:, j : j + 1],
+                    in1=acc[g][k][:],
+                    op0=ALU.mult,
+                    op1=ALU.add,
+                    accum_out=row_sum[g][:, k : k + 1],
+                )
+                nc.gpsimd.tensor_tensor(out=y[g][:, k, :], in0=y[g][:, k, :], in1=c[:], op=ALU.add)
+
+        def mean(g):
+            neg_mean[g] = small.tile([P, GROUP], F32, name="neg_mean")
+            nc.vector.tensor_scalar(
+                out=neg_mean[g][:],
+                in0=row_sum[g][:],
+                scalar1=c_sum[:, 0:1],
+                scalar2=-1.0 / FEAT,
+                op0=ALU.add,
+                op1=ALU.mult,
+            )
+
+        def deviation(g):
+            sq_sum = small.tile([P, GROUP], F32, name="sq_sum")
+            for k in range(GROUP):
+                squares = small.tile([P, FEAT], BF16, name="squares")
+                nc.scalar.activation(
+                    out=squares[:],
+                    in_=y[g][:, k, :],
+                    func=ACT.Square,
+                    bias=neg_mean[g][:, k : k + 1],
+                    scale=1.0,
+                    accum_out=sq_sum[:, k : k + 1],
+                )
+            std[g] = small.tile([P, GROUP], F32, name="std")
+            nc.scalar.activation(out=std[g][:], in_=sq_sum[:], func=ACT.Sqrt, bias=eps[:, 0:1], scale=1.0 / FEAT)
+
+        def centre_and_gain(g):
+            res[g] = back.tile([P, GROUP, FEAT], F32, name="res")
+            for k in range(GROUP):
+                nc.vector.scalar_tensor_tensor(
+                    out=res[g][:, k, :],
+                    in0=y[g][:, k, :],
+                    scalar=neg_mean[g][:, k : k + 1],
+                    in1=gamma_ps[:],
+                    op0=ALU.add,
+                    op1=ALU.mult,
+                )
+
+        def normalise_and_store(g):
+            rstd = small.tile([P, GROUP], F32, name="rstd")
+            nc.vector.reciprocal(out=rstd[:], in_=std[g][:])
+            for k in range(GROUP):
+                nc.vector.scalar_tensor_tensor(
+                    out=res[g][:, k, :],
+                    in0=res[g][:, k, :],
+                    scalar=rstd[:, k : k + 1],
+                    in1=beta_ps[:],
+                    op0=ALU.mult,
+                    op1=ALU.add,
+                )
+                nc.sync.dma_start(out=out_rows[:, g * GROUP + k, :], in_=res[g][:, k, :])
+
+        node_t = psum_t.tile([P, PAIR, PACK, P], BF16, name="xt")
+        for t in range(PACK):
+            nc.tensor.transpose(node_t[:, 0, t, :], node_sb[:, t * P : (t + 1) * P], ident[:])
+        node_grouped = consts.tile([P, GRAPHS, NODES, PACK], BF16, name="node_grouped", align_bytes=64)
+        nc.vector.tensor_copy(
+            out=node_grouped[:], in_=node_t[:, 0, :, :].rearrange("p t (b n) -> p b n t", b=GRAPHS)
+        )
+        col_grouped = consts.tile([P, NODES, GRAPHS, REP, PACK], BF16, name="col_grouped", align_bytes=64)
+        for b in range(GRAPHS):
+            nc.vector.tensor_copy(
+                out=col_grouped[:, :, b, :, :],
+                in_=node_grouped[:, b, :, :].unsqueeze(2).to_broadcast([P, NODES, REP, PACK]),
+            )
+        node_codes = consts.tile([P, P], U32, name="node_codes", align_bytes=64)
+        node_scales = consts.tile([P, P], U8, name="node_scales", align_bytes=64)
+        nc.vector.quantize_mx(
+            out=node_codes[:].bitcast(FP8X4),
+            scales=node_scales[:],
+            in_=node_grouped[:].rearrange("p b n t -> p (b n t)"),
+        )
+
+        mask_and_transpose(0)
+
         w_codes = consts.tile([P, 3, FEAT], U32, name="w_codes", align_bytes=64)
         w_scales = consts.tile([P, 3, FEAT], U8, name="w_scales", align_bytes=64)
-        w_grouped = []
-        for blk in (2, 1, 0):
-            w_raw = w_stage.tile([P, PACK, FEAT], BF16, name="w_raw")
-            nc.sync.dma_start(
-                out=w_raw[:],
-                in_=Wedge[blk * FEAT : (blk + 1) * FEAT, :].rearrange("(t p) n -> p t n", p=P),
+        w_grouped = {}
+
+        def regroup_w(blk):
+            w_grouped[blk] = w_stage.tile([P, FEAT, PACK], BF16, name="w_grouped", align_bytes=64)
+            nc.vector.tensor_copy(
+                out=w_grouped[blk][:].rearrange("p (n i) t -> p n t i", i=4),
+                in_=w_raw[blk][:].rearrange("p t (n i) -> p n t i", i=4),
             )
-            grouped_w = w_stage.tile([P, FEAT, PACK], BF16, name="grouped_w", align_bytes=64)
-            nc.vector.tensor_copy(out=grouped_w[:], in_=w_raw[:].rearrange("p t n -> p n t"))
-            w_grouped.append((blk, grouped_w))
-        for blk, grouped_w in w_grouped:
+
+        def quantise_w(blk):
             nc.vector.quantize_mx(
                 out=w_codes[:, blk, :].bitcast(FP8X4),
                 scales=w_scales[:, blk, :],
-                in_=grouped_w[:].rearrange("p n t -> p (n t)"),
+                in_=w_grouped[blk][:].rearrange("p n t -> p (n t)"),
             )
+
+        col4_codes = consts.tile([P, NODES * GRAPHS, REP], U32, name="col4_codes", align_bytes=64)
+        col4_scales = consts.tile([P, NODES * GRAPHS, REP], U8, name="col4_scales", align_bytes=64)
+        nc.vector.memset(col4_scales[:].bitcast(I32), 0)
+        regroup_w(2)
+        regroup_w(1)
+        quantise_w(2)
+        regroup_w(0)
+        quantise_w(1)
+        nc.vector.quantize_mx(
+            out=col4_codes[:].rearrange("p a r -> p (a r)").bitcast(FP8X4),
+            scales=col4_scales[:].rearrange("p a r -> p (a r)"),
+            in_=col_grouped[:].rearrange("p j b r t -> p (j b r t)"),
+        )
+        quantise_w(0)
 
         gamma_ps = psum_const.tile([P, FEAT], F32, name="gamma_ps")
         nc.tensor.matmul(out=gamma_ps[:], lhsT=ones[:], rhs=vec_rows[:, 0, :], start=True, stop=True)
@@ -96,51 +287,7 @@ def tile_densegatlayer_pb_kernel(
         bias_all = consts.tile([P, FEAT], F32, name="bias_all")
         nc.vector.tensor_copy(out=bias_all[:], in_=bias_ps[:])
 
-        node_t = psum_t.tile([P, PAIR, PACK, P], BF16, name="xt")
-        for t in range(PACK):
-            nc.tensor.transpose(node_t[:, 0, t, :], node_sb[:, t * P : (t + 1) * P], ident[:])
-        node_grouped = consts.tile([P, P, PACK], BF16, name="node_grouped", align_bytes=64)
-        nc.vector.tensor_copy(out=node_grouped[:], in_=node_t[:, 0, :, :].rearrange("p t n -> p n t"))
-        col_grouped = consts.tile([P, NODES, GRAPHS, REP, PACK], BF16, name="col_grouped", align_bytes=64)
-        for b in range(GRAPHS):
-            nc.vector.tensor_copy(
-                out=col_grouped[:, :, b, :, :],
-                in_=node_t[:, 0, :, b * NODES : (b + 1) * NODES]
-                .rearrange("p t j -> p j t")
-                .unsqueeze(2)
-                .to_broadcast([P, NODES, REP, PACK]),
-            )
-        node_codes = consts.tile([P, P], U32, name="node_codes", align_bytes=64)
-        node_scales = consts.tile([P, P], U8, name="node_scales", align_bytes=64)
-        nc.vector.quantize_mx(
-            out=node_codes[:].bitcast(FP8X4),
-            scales=node_scales[:],
-            in_=node_grouped[:].rearrange("p n t -> p (n t)"),
-        )
-        col4_codes = consts.tile([P, NODES * GRAPHS, REP], U32, name="col4_codes", align_bytes=64)
-        col4_scales = consts.tile([P, NODES * GRAPHS, REP], U8, name="col4_scales", align_bytes=64)
-        nc.vector.memset(col4_scales[:].bitcast(I32), 0)
-        nc.vector.quantize_mx(
-            out=col4_codes[:].rearrange("p a r -> p (a r)").bitcast(FP8X4),
-            scales=col4_scales[:].rearrange("p a r -> p (a r)"),
-            in_=col_grouped[:].rearrange("p j b r t -> p (j b r t)"),
-        )
-        col_codes = consts.tile([P, NODES, P], U32, name="col_codes", align_bytes=64)
-        col_scales = consts.tile([P, NODES, P], U8, name="col_scales", align_bytes=64)
-        nc.vector.tensor_copy(
-            out=col_scales[:].bitcast(I32).rearrange("p j (b s) -> p (j b) s", b=GRAPHS),
-            in_=col4_scales[:].bitcast(I32).to_broadcast([P, NODES * GRAPHS, NODES // REP]),
-        )
-        for q in range(4):
-            js = slice(q * NODES // 4, (q + 1) * NODES // 4)
-            ab = slice(q * NODES * GRAPHS // 4, (q + 1) * NODES * GRAPHS // 4)
-            nc.vector.tensor_copy(
-                out=col_codes[:, js, :].bitcast(I32).rearrange("p j (b s r) -> p (j b) s r", b=GRAPHS, r=REP),
-                in_=col4_codes[:, ab, :]
-                .bitcast(I32)
-                .unsqueeze(2)
-                .to_broadcast([P, NODES * GRAPHS // 4, NODES // REP, REP]),
-            )
+        mask_and_transpose(1)
 
         row_ps = psum_acc.tile([P, FEAT], F32, name="acc")
         nc.tensor.matmul_mx(
@@ -152,115 +299,29 @@ def tile_densegatlayer_pb_kernel(
             start=True,
             stop=True,
         )
+        quantise(0)
         c = consts.tile([P, FEAT], F32, name="c")
         c_sum = consts.tile([P, 1], F32, name="c_sum")
         nc.vector.scalar_tensor_tensor(
             out=c[:], in0=row_ps[:], scalar=1.0, in1=bias_all[:], op0=ALU.mult, op1=ALU.add, accum_out=c_sum[:]
         )
+        products(0)
 
-        for g in range(NODES // GROUP):
-            j0 = g * GROUP
-            emb_sb = emb_pool.tile([P, GROUP, FEAT], BF16, name="emb_sb")
-            nc.sync.dma_start(out=emb_sb[:], in_=emb_rows[:, j0 : j0 + GROUP, :])
-
-            xe_bf = front.tile([P, GROUP, FEAT], BF16, name="xe_bf")
-            for k in range(GROUP):
-                nc.scalar.activation(
-                    out=xe_bf[:, k, :], in_=emb_sb[:, k, :], func=ACT.Copy, scale=e_mask[:, j0 + k : j0 + k + 1]
-                )
-            grouped = front.tile([P, GROUP, P, PACK], BF16, name="grouped", align_bytes=64)
-            for h in range(GROUP // PAIR):
-                xt = psum_t.tile([P, PAIR, PACK, P], BF16, name="xt")
-                for k in range(PAIR):
-                    for t in range(PACK):
-                        nc.tensor.transpose(xt[:, k, t, :], xe_bf[:, h * PAIR + k, t * P : (t + 1) * P], ident[:])
-                nc.scalar.copy(
-                    out=grouped[:, h * PAIR : (h + 1) * PAIR, :, :], in_=xt[:].rearrange("p k t r -> p k r t")
-                )
-            codes = front.tile([P, GROUP, P], U32, name="codes", align_bytes=64)
-            scales = front.tile([P, GROUP, P], U8, name="scales", align_bytes=64)
-            nc.vector.quantize_mx(
-                out=codes[:].rearrange("p k r -> p (k r)").bitcast(FP8X4),
-                scales=scales[:].rearrange("p k r -> p (k r)"),
-                in_=grouped[:].rearrange("p k r t -> p (k r t)"),
-            )
-
-            y = back.tile([P, GROUP, FEAT], F32, name="y")
-            row_sum = small.tile([P, GROUP], F32, name="row_sum")
-            for k in range(GROUP):
-                j = j0 + k
-                acc = psum_acc.tile([P, FEAT], F32, name="acc")
-                nc.tensor.matmul_mx(
-                    out=acc[:],
-                    lhsT=codes[:, k, :].bitcast(FP8X4),
-                    lhsT_scale=scales[:, k, :],
-                    rhs=w_codes[:, 2, :].bitcast(FP8X4),
-                    rhs_scale=w_scales[:, 2, :],
-                    start=True,
-                    stop=False,
-                )
-                nc.tensor.matmul_mx(
-                    out=acc[:],
-                    lhsT=col_codes[:, j, :].bitcast(FP8X4),
-                    lhsT_scale=col_scales[:, j, :],
-                    rhs=w_codes[:, 1, :].bitcast(FP8X4),
-                    rhs_scale=w_scales[:, 1, :],
-                    start=False,
-                    stop=True,
-                )
-                nc.vector.scalar_tensor_tensor(
-                    out=y[:, k, :],
-                    in0=emb_sb[:, k, :],
-                    scalar=e_mask[:, j : j + 1],
-                    in1=acc[:],
-                    op0=ALU.mult,
-                    op1=ALU.add,
-                    accum_out=row_sum[:, k : k + 1],
-                )
-                nc.gpsimd.tensor_tensor(out=y[:, k, :], in0=y[:, k, :], in1=c[:], op=ALU.add)
-
-            neg_mean = small.tile([P, GROUP], F32, name="neg_mean")
-            nc.vector.tensor_scalar(
-                out=neg_mean[:],
-                in0=row_sum[:],
-                scalar1=c_sum[:, 0:1],
-                scalar2=-1.0 / FEAT,
-                op0=ALU.add,
-                op1=ALU.mult,
-            )
-            sq_sum = small.tile([P, GROUP], F32, name="sq_sum")
-            for k in range(GROUP):
-                squares = small.tile([P, FEAT], BF16, name="squares")
-                nc.scalar.activation(
-                    out=squares[:],
-                    in_=y[:, k, :],
-                    func=ACT.Square,
-                    bias=neg_mean[:, k : k + 1],
-                    scale=1.0,
-                    accum_out=sq_sum[:, k : k + 1],
-                )
-            std = small.tile([P, GROUP], F32, name="std")
-            nc.scalar.activation(out=std[:], in_=sq_sum[:], func=ACT.Sqrt, bias=eps[:, 0:1], scale=1.0 / FEAT)
-            rstd = small.tile([P, GROUP], F32, name="rstd")
-            nc.vector.reciprocal(out=rstd[:], in_=std[:])
-
-            res = back.tile([P, GROUP, FEAT], F32, name="res")
-            for k in range(GROUP):
-                nc.vector.scalar_tensor_tensor(
-                    out=res[:, k, :],
-                    in0=y[:, k, :],
-                    scalar=neg_mean[:, k : k + 1],
-                    in1=gamma_ps[:],
-                    op0=ALU.add,
-                    op1=ALU.mult,
-                )
-            for k in range(GROUP):
-                nc.vector.scalar_tensor_tensor(
-                    out=res[:, k, :],
-                    in0=res[:, k, :],
-                    scalar=rstd[:, k : k + 1],
-                    in1=beta_ps[:],
-                    op0=ALU.mult,
-                    op1=ALU.add,
-                )
-            nc.sync.dma_start(out=out_rows[:, j0 : j0 + GROUP, :], in_=res[:])
+        for i in range(N_GROUPS + 1):
+            if i + LOADS_AHEAD < N_GROUPS:
+                load(i + LOADS_AHEAD)
+            if i < N_GROUPS:
+                residual(i)
+            if i + 1 < N_GROUPS:
+                quantise(i + 1)
+            if i < N_GROUPS:
+                mean(i)
+            if i + 2 < N_GROUPS:
+                mask_and_transpose(i + 2)
+            if i + 1 < N_GROUPS:
+                products(i + 1)
+            if i >= 1:
+                normalise_and_store(i - 1)
+            if i < N_GROUPS:
+                deviation(i)
+                centre_and_gain(i)

@@ -19,6 +19,7 @@ GROUP = 4
 N_GROUPS = NODES // GROUP
 PAIR = 2
 REP = 4
+GPSIMD_TILES = 3
 LOADS_AHEAD = 4
 LN_EPS = 1e-5
 
@@ -168,7 +169,12 @@ def tile_densegatlayer_pb_kernel(
                     op1=ALU.add,
                     accum_out=row_sum[g][:, k : k + 1],
                 )
-                nc.gpsimd.tensor_tensor(out=y[g][:, k, :], in0=y[g][:, k, :], in1=c[:], op=ALU.add)
+                if k < GPSIMD_TILES:
+                    nc.gpsimd.tensor_tensor(out=y[g][:, k, :], in0=y[g][:, k, :], in1=c[:], op=ALU.add)
+
+        def residual_rest(g):
+            for k in range(GPSIMD_TILES, GROUP):
+                nc.vector.tensor_tensor(out=y[g][:, k, :], in0=y[g][:, k, :], in1=c[:], op=ALU.add)
 
         def mean(g):
             neg_mean[g] = small.tile([P, GROUP], F32, name="neg_mean")
@@ -315,6 +321,7 @@ def tile_densegatlayer_pb_kernel(
             if i + 1 < N_GROUPS:
                 quantise(i + 1)
             if i < N_GROUPS:
+                residual_rest(i)
                 mean(i)
             if i + 2 < N_GROUPS:
                 mask_and_transpose(i + 2)

@@ -19,7 +19,7 @@ GROUP = 4
 N_GROUPS = NODES // GROUP
 PAIR = 2
 REP = 4
-GPSIMD_TILES = 3
+HANDED_OVER = 1
 LOADS_AHEAD = 4
 LN_EPS = 1e-5
 
@@ -45,8 +45,8 @@ def tile_densegatlayer_pb_kernel(
         tc.psum_pool(name="psum_acc", bufs=GROUP) as psum_acc,
         tc.manual_schedule(),
     ):
-        emb_sb, grouped, codes, scales, col_codes, col_scales = {}, {}, {}, {}, {}, {}
-        acc, y, row_sum, neg_mean, std, res = {}, {}, {}, {}, {}, {}
+        emb_sb, grouped, codes, scales = {}, {}, {}, {}
+        acc, y, row_sum, neg_mean, rstd, res = {}, {}, {}, {}, {}, {}
 
         def load(g):
             emb_sb[g] = emb_pool.tile([P, GROUP, FEAT], BF16, name="emb_sb")
@@ -84,7 +84,7 @@ def tile_densegatlayer_pb_kernel(
         eps = consts.tile([P, 1], F32, name="eps")
         nc.vector.memset(eps[:], LN_EPS)
         warm = consts.tile([P, 1], F32, name="warm")
-        nc.scalar.activation(out=warm[:], in_=eps[:], func=ACT.Sqrt)
+        nc.scalar.activation(out=warm[:], in_=eps[:], func=ACT.Abs_reciprocal_sqrt)
 
         mask_col = consts.tile([P, 1], F32, name="mask_col")
         nc.vector.tensor_copy(out=mask_col[:], in_=mask_col_bf[:])
@@ -116,20 +116,6 @@ def tile_densegatlayer_pb_kernel(
                 scales=scales[g][:].rearrange("p k r -> p (k r)"),
                 in_=grouped[g][:].rearrange("p k r t -> p (k r t)"),
             )
-            col_codes[g] = front.tile([P, GROUP, P], U32, name="col_codes", align_bytes=64)
-            col_scales[g] = front.tile([P, GROUP, P], U8, name="col_scales", align_bytes=64)
-            pairs = slice(g * GROUP * GRAPHS, (g + 1) * GROUP * GRAPHS)
-            nc.vector.tensor_copy(
-                out=col_codes[g][:].bitcast(I32).rearrange("p k (b s r) -> p (k b) s r", b=GRAPHS, r=REP),
-                in_=col4_codes[:, pairs, :]
-                .bitcast(I32)
-                .unsqueeze(2)
-                .to_broadcast([P, GROUP * GRAPHS, NODES // REP, REP]),
-            )
-            nc.vector.tensor_copy(
-                out=col_scales[g][:].bitcast(I32).rearrange("p k (b s) -> p (k b) s", b=GRAPHS),
-                in_=col4_scales[:, pairs, :].bitcast(I32).to_broadcast([P, GROUP * GRAPHS, NODES // REP]),
-            )
 
         def products(g):
             acc[g] = []
@@ -146,8 +132,8 @@ def tile_densegatlayer_pb_kernel(
                 )
                 nc.tensor.matmul_mx(
                     out=bank[:],
-                    lhsT=col_codes[g][:, k, :].bitcast(FP8X4),
-                    lhsT_scale=col_scales[g][:, k, :],
+                    lhsT=col_codes[:, g * GROUP + k, :].bitcast(FP8X4),
+                    lhsT_scale=col_scales[:, g * GROUP + k, :],
                     rhs=w_codes[:, 1, :].bitcast(FP8X4),
                     rhs_scale=w_scales[:, 1, :],
                     start=False,
@@ -158,7 +144,7 @@ def tile_densegatlayer_pb_kernel(
         def residual(g):
             y[g] = back.tile([P, GROUP, FEAT], F32, name="y")
             row_sum[g] = small.tile([P, GROUP], F32, name="row_sum")
-            for k in range(GROUP):
+            for k in reversed(range(GROUP)):
                 j = g * GROUP + k
                 nc.vector.scalar_tensor_tensor(
                     out=y[g][:, k, :],
@@ -169,22 +155,14 @@ def tile_densegatlayer_pb_kernel(
                     op1=ALU.add,
                     accum_out=row_sum[g][:, k : k + 1],
                 )
-                if k < GPSIMD_TILES:
-                    nc.gpsimd.tensor_tensor(out=y[g][:, k, :], in0=y[g][:, k, :], in1=c[:], op=ALU.add)
-
-        def residual_rest(g):
-            for k in range(GPSIMD_TILES, GROUP):
-                nc.vector.tensor_tensor(out=y[g][:, k, :], in0=y[g][:, k, :], in1=c[:], op=ALU.add)
+            nc.gpsimd.tensor_tensor(
+                out=y[g][:], in0=y[g][:], in1=c[:].unsqueeze(1).to_broadcast([P, GROUP, FEAT]), op=ALU.add
+            )
 
         def mean(g):
             neg_mean[g] = small.tile([P, GROUP], F32, name="neg_mean")
-            nc.vector.tensor_scalar(
-                out=neg_mean[g][:],
-                in0=row_sum[g][:],
-                scalar1=c_sum[:, 0:1],
-                scalar2=-1.0 / FEAT,
-                op0=ALU.add,
-                op1=ALU.mult,
+            nc.scalar.activation(
+                out=neg_mean[g][:], in_=row_sum[g][:], func=ACT.Identity, bias=neg_c_mean[:, 0:1], scale=-1.0 / FEAT
             )
 
         def deviation(g):
@@ -199,8 +177,10 @@ def tile_densegatlayer_pb_kernel(
                     scale=1.0,
                     accum_out=sq_sum[:, k : k + 1],
                 )
-            std[g] = small.tile([P, GROUP], F32, name="std")
-            nc.scalar.activation(out=std[g][:], in_=sq_sum[:], func=ACT.Sqrt, bias=eps[:, 0:1], scale=1.0 / FEAT)
+            rstd[g] = small.tile([P, GROUP], F32, name="rstd")
+            nc.scalar.activation(
+                out=rstd[g][:], in_=sq_sum[:], func=ACT.Abs_reciprocal_sqrt, bias=eps[:, 0:1], scale=1.0 / FEAT
+            )
 
         def centre_and_gain(g):
             res[g] = back.tile([P, GROUP, FEAT], F32, name="res")
@@ -214,19 +194,33 @@ def tile_densegatlayer_pb_kernel(
                     op1=ALU.mult,
                 )
 
-        def normalise_and_store(g):
-            rstd = small.tile([P, GROUP], F32, name="rstd")
-            nc.vector.reciprocal(out=rstd[:], in_=std[g][:])
-            for k in range(GROUP):
+        def store(g, k):
+            nc.sync.dma_start(out=out_rows[:, g * GROUP + k, :], in_=res[g][:, k, :])
+
+        def normalise_handed_over(g):
+            for k in range(HANDED_OVER):
+                nc.gpsimd.tensor_scalar(
+                    out=res[g][:, k, :],
+                    in0=res[g][:, k, :],
+                    scalar1=rstd[g][:, k : k + 1],
+                    scalar2=0.0,
+                    op0=ALU.mult,
+                    op1=ALU.add,
+                )
+                nc.gpsimd.tensor_tensor(out=res[g][:, k, :], in0=res[g][:, k, :], in1=beta_sb[:], op=ALU.add)
+                store(g, k)
+
+        def normalise(g):
+            for k in range(HANDED_OVER, GROUP):
                 nc.vector.scalar_tensor_tensor(
                     out=res[g][:, k, :],
                     in0=res[g][:, k, :],
-                    scalar=rstd[:, k : k + 1],
+                    scalar=rstd[g][:, k : k + 1],
                     in1=beta_ps[:],
                     op0=ALU.mult,
                     op1=ALU.add,
                 )
-                nc.sync.dma_start(out=out_rows[:, g * GROUP + k, :], in_=res[g][:, k, :])
+                store(g, k)
 
         node_t = psum_t.tile([P, PAIR, PACK, P], BF16, name="xt")
         for t in range(PACK):
@@ -283,6 +277,16 @@ def tile_densegatlayer_pb_kernel(
             in_=col_grouped[:].rearrange("p j b r t -> p (j b r t)"),
         )
         quantise_w(0)
+        col_codes = consts.tile([P, NODES, P], U32, name="col_codes", align_bytes=64)
+        col_scales = consts.tile([P, NODES, P], U8, name="col_scales", align_bytes=64)
+        nc.vector.tensor_copy(
+            out=col_scales[:].bitcast(I32).rearrange("p j (b s) -> p (j b) s", b=GRAPHS),
+            in_=col4_scales[:].bitcast(I32).to_broadcast([P, NODES * GRAPHS, NODES // REP]),
+        )
+        nc.vector.tensor_copy(
+            out=col_codes[:].bitcast(I32).rearrange("p j (b s r) -> p (j b) s r", b=GRAPHS, r=REP),
+            in_=col4_codes[:].bitcast(I32).unsqueeze(2).to_broadcast([P, NODES * GRAPHS, NODES // REP, REP]),
+        )
 
         gamma_ps = psum_const.tile([P, FEAT], F32, name="gamma_ps")
         nc.tensor.matmul(out=gamma_ps[:], lhsT=ones[:], rhs=vec_rows[:, 0, :], start=True, stop=True)
@@ -292,6 +296,8 @@ def tile_densegatlayer_pb_kernel(
         nc.tensor.matmul(out=bias_ps[:], lhsT=ones[:], rhs=vec_rows[:, 2, :], start=True, stop=True)
         bias_all = consts.tile([P, FEAT], F32, name="bias_all")
         nc.vector.tensor_copy(out=bias_all[:], in_=bias_ps[:])
+        beta_sb = consts.tile([P, FEAT], F32, name="beta_sb")
+        nc.scalar.copy(out=beta_sb[:], in_=beta_ps[:])
 
         mask_and_transpose(1)
 
@@ -311,24 +317,30 @@ def tile_densegatlayer_pb_kernel(
         nc.vector.scalar_tensor_tensor(
             out=c[:], in0=row_ps[:], scalar=1.0, in1=bias_all[:], op0=ALU.mult, op1=ALU.add, accum_out=c_sum[:]
         )
+        neg_c_mean = consts.tile([P, 1], F32, name="neg_c_mean")
+        nc.vector.tensor_scalar_mul(out=neg_c_mean[:], in0=c_sum[:], scalar1=-1.0 / FEAT)
         products(0)
 
-        for i in range(N_GROUPS + 1):
-            if i + LOADS_AHEAD < N_GROUPS:
+        def in_range(g):
+            return 0 <= g < N_GROUPS
+
+        for i in range(N_GROUPS + 2):
+            if in_range(i + LOADS_AHEAD):
                 load(i + LOADS_AHEAD)
-            if i < N_GROUPS:
+            if in_range(i - 2):
+                normalise_handed_over(i - 2)
+            if in_range(i):
                 residual(i)
-            if i + 1 < N_GROUPS:
+            if in_range(i + 1):
                 quantise(i + 1)
-            if i < N_GROUPS:
-                residual_rest(i)
-                mean(i)
-            if i + 2 < N_GROUPS:
+            if in_range(i - 1):
+                mean(i - 1)
+            if in_range(i + 2):
                 mask_and_transpose(i + 2)
-            if i + 1 < N_GROUPS:
+            if in_range(i + 1):
                 products(i + 1)
-            if i >= 1:
-                normalise_and_store(i - 1)
-            if i < N_GROUPS:
-                deviation(i)
-                centre_and_gain(i)
+            if in_range(i - 1):
+                centre_and_gain(i - 1)
+                deviation(i - 1)
+            if in_range(i - 2):
+                normalise(i - 2)

@@ -45,7 +45,7 @@ def tile_densegatlayer_pb_kernel(
         tc.psum_pool(name="psum_acc", bufs=GROUP) as psum_acc,
         tc.manual_schedule(),
     ):
-        emb_sb, grouped, codes, scales = {}, {}, {}, {}
+        emb_sb, xe_bf, xt, grouped, codes, scales = {}, {}, {}, {}, {}, {}
         acc, y, row_sum, neg_mean, rstd, res = {}, {}, {}, {}, {}, {}
 
         def load(g):
@@ -53,15 +53,15 @@ def tile_densegatlayer_pb_kernel(
             nc.sync.dma_start(out=emb_sb[g][:], in_=emb_rows[:, g * GROUP : (g + 1) * GROUP, :])
 
         mask_col_bf = consts.tile([P, 1], BF16, name="mask_col_bf")
-        nc.scalar.dma_start(out=mask_col_bf[:], in_=node_mask.rearrange("b (n o) -> (b n) o", o=1))
+        nc.sync.dma_start(out=mask_col_bf[:], in_=node_mask.rearrange("b (n o) -> (b n) o", o=1))
         mask_row = consts.tile([P, NODES], BF16, name="mask_row")
         for b in range(GRAPHS):
-            nc.scalar.dma_start(
+            nc.sync.dma_start(
                 out=mask_row[b * NODES : (b + 1) * NODES, :],
                 in_=node_mask[b : b + 1, :].rearrange("o n -> (o n)").partition_broadcast(NODES),
             )
         node_sb = consts.tile([P, FEAT], BF16, name="node_sb")
-        nc.scalar.dma_start(out=node_sb[:], in_=new_node.rearrange("b n f -> (b n) f"))
+        nc.sync.dma_start(out=node_sb[:], in_=new_node.rearrange("b n f -> (b n) f"))
         load(0)
         w_raw = {}
         for blk in (2, 1, 0):
@@ -91,21 +91,31 @@ def tile_densegatlayer_pb_kernel(
         e_mask = consts.tile([P, NODES], F32, name="e_mask")
         nc.vector.tensor_scalar_mul(out=e_mask[:], in0=mask_row[:], scalar1=mask_col[:, 0:1])
 
-        def mask_and_transpose(g):
-            xe_bf = front.tile([P, GROUP, FEAT], BF16, name="xe_bf")
+        def mask(g):
+            xe_bf[g] = front.tile([P, GROUP, FEAT], BF16, name="xe_bf")
             for k in range(GROUP):
                 j = g * GROUP + k
                 nc.scalar.activation(
-                    out=xe_bf[:, k, :], in_=emb_sb[g][:, k, :], func=ACT.Copy, scale=e_mask[:, j : j + 1]
+                    out=xe_bf[g][:, k, :], in_=emb_sb[g][:, k, :], func=ACT.Copy, scale=e_mask[:, j : j + 1]
                 )
-            grouped[g] = front.tile([P, GROUP, P, PACK], BF16, name="grouped", align_bytes=64)
+
+        def transpose(g):
+            xt[g] = []
             for h in range(GROUP // PAIR):
-                xt = psum_t.tile([P, PAIR, PACK, P], BF16, name="xt")
+                bank = psum_t.tile([P, PAIR, PACK, P], BF16, name="xt")
                 for k in range(PAIR):
                     for t in range(PACK):
-                        nc.tensor.transpose(xt[:, k, t, :], xe_bf[:, h * PAIR + k, t * P : (t + 1) * P], ident[:])
+                        nc.tensor.transpose(
+                            bank[:, k, t, :], xe_bf[g][:, h * PAIR + k, t * P : (t + 1) * P], ident[:]
+                        )
+                xt[g].append(bank)
+
+        def unload(g):
+            grouped[g] = front.tile([P, GROUP, P, PACK], BF16, name="grouped", align_bytes=64)
+            for h in range(GROUP // PAIR):
                 nc.scalar.copy(
-                    out=grouped[g][:, h * PAIR : (h + 1) * PAIR, :, :], in_=xt[:].rearrange("p k t r -> p k r t")
+                    out=grouped[g][:, h * PAIR : (h + 1) * PAIR, :, :],
+                    in_=xt[g][h][:].rearrange("p k t r -> p k r t"),
                 )
 
         def quantise(g):
@@ -182,9 +192,23 @@ def tile_densegatlayer_pb_kernel(
                 out=rstd[g][:], in_=sq_sum[:], func=ACT.Abs_reciprocal_sqrt, bias=eps[:, 0:1], scale=1.0 / FEAT
             )
 
+        def standardise_handed_over(g):
+            for k in range(HANDED_OVER):
+                shift = small.tile([P, 1], F32, name="shift")
+                nc.scalar.activation(
+                    out=shift[:], in_=neg_mean[g][:, k : k + 1], func=ACT.Copy, scale=rstd[g][:, k : k + 1]
+                )
+                nc.scalar.activation(
+                    out=res[g][:, k, :],
+                    in_=y[g][:, k, :],
+                    func=ACT.Identity,
+                    bias=shift[:, 0:1],
+                    scale=rstd[g][:, k : k + 1],
+                )
+
         def centre_and_gain(g):
             res[g] = back.tile([P, GROUP, FEAT], F32, name="res")
-            for k in range(GROUP):
+            for k in range(HANDED_OVER, GROUP):
                 nc.vector.scalar_tensor_tensor(
                     out=res[g][:, k, :],
                     in0=y[g][:, k, :],
@@ -199,14 +223,7 @@ def tile_densegatlayer_pb_kernel(
 
         def normalise_handed_over(g):
             for k in range(HANDED_OVER):
-                nc.gpsimd.tensor_scalar(
-                    out=res[g][:, k, :],
-                    in0=res[g][:, k, :],
-                    scalar1=rstd[g][:, k : k + 1],
-                    scalar2=0.0,
-                    op0=ALU.mult,
-                    op1=ALU.add,
-                )
+                nc.gpsimd.tensor_tensor(out=res[g][:, k, :], in0=res[g][:, k, :], in1=gamma_sb[:], op=ALU.mult)
                 nc.gpsimd.tensor_tensor(out=res[g][:, k, :], in0=res[g][:, k, :], in1=beta_sb[:], op=ALU.add)
                 store(g, k)
 
@@ -222,36 +239,13 @@ def tile_densegatlayer_pb_kernel(
                 )
                 store(g, k)
 
-        node_t = psum_t.tile([P, PAIR, PACK, P], BF16, name="xt")
-        for t in range(PACK):
-            nc.tensor.transpose(node_t[:, 0, t, :], node_sb[:, t * P : (t + 1) * P], ident[:])
-        node_grouped = consts.tile([P, GRAPHS, NODES, PACK], BF16, name="node_grouped", align_bytes=64)
-        nc.vector.tensor_copy(
-            out=node_grouped[:], in_=node_t[:, 0, :, :].rearrange("p t (b n) -> p b n t", b=GRAPHS)
-        )
-        col_grouped = consts.tile([P, NODES, GRAPHS, REP, PACK], BF16, name="col_grouped", align_bytes=64)
-        for b in range(GRAPHS):
-            nc.vector.tensor_copy(
-                out=col_grouped[:, :, b, :, :],
-                in_=node_grouped[:, b, :, :].unsqueeze(2).to_broadcast([P, NODES, REP, PACK]),
-            )
-        node_codes = consts.tile([P, P], U32, name="node_codes", align_bytes=64)
-        node_scales = consts.tile([P, P], U8, name="node_scales", align_bytes=64)
-        nc.vector.quantize_mx(
-            out=node_codes[:].bitcast(FP8X4),
-            scales=node_scales[:],
-            in_=node_grouped[:].rearrange("p b n t -> p (b n t)"),
-        )
-
-        mask_and_transpose(0)
-
         w_codes = consts.tile([P, 3, FEAT], U32, name="w_codes", align_bytes=64)
         w_scales = consts.tile([P, 3, FEAT], U8, name="w_scales", align_bytes=64)
         w_grouped = {}
 
-        def regroup_w(blk):
+        def regroup_w(blk, copy):
             w_grouped[blk] = w_stage.tile([P, FEAT, PACK], BF16, name="w_grouped", align_bytes=64)
-            nc.vector.tensor_copy(
+            copy(
                 out=w_grouped[blk][:].rearrange("p (n i) t -> p n t i", i=4),
                 in_=w_raw[blk][:].rearrange("p t (n i) -> p n t i", i=4),
             )
@@ -266,42 +260,72 @@ def tile_densegatlayer_pb_kernel(
         col4_codes = consts.tile([P, NODES * GRAPHS, REP], U32, name="col4_codes", align_bytes=64)
         col4_scales = consts.tile([P, NODES * GRAPHS, REP], U8, name="col4_scales", align_bytes=64)
         nc.vector.memset(col4_scales[:].bitcast(I32), 0)
-        regroup_w(2)
-        regroup_w(1)
+        col_codes = consts.tile([P, NODES, P], U32, name="col_codes", align_bytes=64)
+        col_scales = consts.tile([P, NODES, P], U8, name="col_scales", align_bytes=64)
+
+        def repeat_codes(g0, g1):
+            j0, j1 = g0 * GROUP, g1 * GROUP
+            nc.vector.tensor_copy(
+                out=col_codes[:, j0:j1, :].bitcast(I32).rearrange("p j (b s r) -> p (j b) s r", b=GRAPHS, r=REP),
+                in_=col4_codes[:, j0 * GRAPHS : j1 * GRAPHS, :]
+                .bitcast(I32)
+                .unsqueeze(2)
+                .to_broadcast([P, (j1 - j0) * GRAPHS, NODES // REP, REP]),
+            )
+
+        node_t = psum_t.tile([P, PAIR, PACK, P], BF16, name="xt")
+        for t in range(PACK):
+            nc.tensor.transpose(node_t[:, 0, t, :], node_sb[:, t * P : (t + 1) * P], ident[:])
+        mask(0)
+        transpose(0)
+        unload(0)
+        mask(1)
+        transpose(1)
+        regroup_w(2, nc.vector.tensor_copy)
+        node_grouped = consts.tile([P, GRAPHS, NODES, PACK], BF16, name="node_grouped", align_bytes=64)
+        nc.vector.tensor_copy(
+            out=node_grouped[:], in_=node_t[:, 0, :, :].rearrange("p t (b n) -> p b n t", b=GRAPHS)
+        )
         quantise_w(2)
-        regroup_w(0)
-        quantise_w(1)
+        col_grouped = consts.tile([P, NODES, GRAPHS, REP, PACK], BF16, name="col_grouped", align_bytes=64)
+        for b in range(GRAPHS):
+            nc.vector.tensor_copy(
+                out=col_grouped[:, :, b, :, :],
+                in_=node_grouped[:, b, :, :].unsqueeze(2).to_broadcast([P, NODES, REP, PACK]),
+            )
+        regroup_w(1, nc.vector.tensor_copy)
         nc.vector.quantize_mx(
             out=col4_codes[:].rearrange("p a r -> p (a r)").bitcast(FP8X4),
             scales=col4_scales[:].rearrange("p a r -> p (a r)"),
             in_=col_grouped[:].rearrange("p j b r t -> p (j b r t)"),
         )
-        quantise_w(0)
-        col_codes = consts.tile([P, NODES, P], U32, name="col_codes", align_bytes=64)
-        col_scales = consts.tile([P, NODES, P], U8, name="col_scales", align_bytes=64)
+        quantise_w(1)
         nc.vector.tensor_copy(
             out=col_scales[:].bitcast(I32).rearrange("p j (b s) -> p (j b) s", b=GRAPHS),
             in_=col4_scales[:].bitcast(I32).to_broadcast([P, NODES * GRAPHS, NODES // REP]),
         )
-        nc.vector.tensor_copy(
-            out=col_codes[:].bitcast(I32).rearrange("p j (b s r) -> p (j b) s r", b=GRAPHS, r=REP),
-            in_=col4_codes[:].bitcast(I32).unsqueeze(2).to_broadcast([P, NODES * GRAPHS, NODES // REP, REP]),
+        repeat_codes(0, 1)
+        quantise(0)
+        products(0)
+        node_codes = consts.tile([P, P], U32, name="node_codes", align_bytes=64)
+        node_scales = consts.tile([P, P], U8, name="node_scales", align_bytes=64)
+        nc.vector.quantize_mx(
+            out=node_codes[:].bitcast(FP8X4),
+            scales=node_scales[:],
+            in_=node_grouped[:].rearrange("p b n t -> p (b n t)"),
         )
+        regroup_w(0, nc.scalar.copy)
+        quantise_w(0)
 
-        gamma_ps = psum_const.tile([P, FEAT], F32, name="gamma_ps")
-        nc.tensor.matmul(out=gamma_ps[:], lhsT=ones[:], rhs=vec_rows[:, 0, :], start=True, stop=True)
-        beta_ps = psum_const.tile([P, FEAT], F32, name="beta_ps")
-        nc.tensor.matmul(out=beta_ps[:], lhsT=ones[:], rhs=vec_rows[:, 1, :], start=True, stop=True)
-        bias_ps = psum_acc.tile([P, FEAT], F32, name="acc")
-        nc.tensor.matmul(out=bias_ps[:], lhsT=ones[:], rhs=vec_rows[:, 2, :], start=True, stop=True)
+        def repeat_vector(v, bank_name):
+            bank = psum_const.tile([P, FEAT], F32, name=bank_name)
+            nc.tensor.matmul(out=bank[:], lhsT=ones[:], rhs=vec_rows[:, v, :], start=True, stop=True)
+            return bank
+
+        bias_ps = repeat_vector(2, "const_a")
         bias_all = consts.tile([P, FEAT], F32, name="bias_all")
-        nc.vector.tensor_copy(out=bias_all[:], in_=bias_ps[:])
-        beta_sb = consts.tile([P, FEAT], F32, name="beta_sb")
-        nc.scalar.copy(out=beta_sb[:], in_=beta_ps[:])
-
-        mask_and_transpose(1)
-
-        row_ps = psum_acc.tile([P, FEAT], F32, name="acc")
+        nc.scalar.copy(out=bias_all[:], in_=bias_ps[:])
+        row_ps = psum_const.tile([P, FEAT], F32, name="const_b")
         nc.tensor.matmul_mx(
             out=row_ps[:],
             lhsT=node_codes[:].bitcast(FP8X4),
@@ -311,7 +335,7 @@ def tile_densegatlayer_pb_kernel(
             start=True,
             stop=True,
         )
-        quantise(0)
+        repeat_codes(1, 2)
         c = consts.tile([P, FEAT], F32, name="c")
         c_sum = consts.tile([P, 1], F32, name="c_sum")
         nc.vector.scalar_tensor_tensor(
@@ -319,7 +343,15 @@ def tile_densegatlayer_pb_kernel(
         )
         neg_c_mean = consts.tile([P, 1], F32, name="neg_c_mean")
         nc.vector.tensor_scalar_mul(out=neg_c_mean[:], in0=c_sum[:], scalar1=-1.0 / FEAT)
-        products(0)
+        gamma_ps = repeat_vector(0, "const_a")
+        beta_ps = repeat_vector(1, "const_b")
+        gamma_sb = consts.tile([P, FEAT], F32, name="gamma_sb")
+        nc.scalar.copy(out=gamma_sb[:], in_=gamma_ps[:])
+        beta_sb = consts.tile([P, FEAT], F32, name="beta_sb")
+        nc.scalar.copy(out=beta_sb[:], in_=beta_ps[:])
+
+        half = 2 + (N_GROUPS - 2) // 2
+        repeated_in_round = {0: (2, half), 1: (half, N_GROUPS)}
 
         def in_range(g):
             return 0 <= g < N_GROUPS
@@ -327,20 +359,25 @@ def tile_densegatlayer_pb_kernel(
         for i in range(N_GROUPS + 2):
             if in_range(i + LOADS_AHEAD):
                 load(i + LOADS_AHEAD)
+            if in_range(i + 1):
+                unload(i + 1)
             if in_range(i - 2):
                 normalise_handed_over(i - 2)
             if in_range(i):
                 residual(i)
             if in_range(i + 1):
                 quantise(i + 1)
+                products(i + 1)
+            if i in repeated_in_round:
+                repeat_codes(*repeated_in_round[i])
             if in_range(i - 1):
                 mean(i - 1)
             if in_range(i + 2):
-                mask_and_transpose(i + 2)
-            if in_range(i + 1):
-                products(i + 1)
+                mask(i + 2)
+                transpose(i + 2)
             if in_range(i - 1):
                 centre_and_gain(i - 1)
                 deviation(i - 1)
+                standardise_handed_over(i - 1)
             if in_range(i - 2):
                 normalise(i - 2)

@@ -192,23 +192,9 @@ def tile_densegatlayer_pb_kernel(
                 out=rstd[g][:], in_=sq_sum[:], func=ACT.Abs_reciprocal_sqrt, bias=eps[:, 0:1], scale=1.0 / FEAT
             )
 
-        def standardise_handed_over(g):
-            for k in range(HANDED_OVER):
-                shift = small.tile([P, 1], F32, name="shift")
-                nc.scalar.activation(
-                    out=shift[:], in_=neg_mean[g][:, k : k + 1], func=ACT.Copy, scale=rstd[g][:, k : k + 1]
-                )
-                nc.scalar.activation(
-                    out=res[g][:, k, :],
-                    in_=y[g][:, k, :],
-                    func=ACT.Identity,
-                    bias=shift[:, 0:1],
-                    scale=rstd[g][:, k : k + 1],
-                )
-
         def centre_and_gain(g):
             res[g] = back.tile([P, GROUP, FEAT], F32, name="res")
-            for k in range(HANDED_OVER, GROUP):
+            for k in range(GROUP):
                 nc.vector.scalar_tensor_tensor(
                     out=res[g][:, k, :],
                     in0=y[g][:, k, :],
@@ -223,7 +209,14 @@ def tile_densegatlayer_pb_kernel(
 
         def normalise_handed_over(g):
             for k in range(HANDED_OVER):
-                nc.gpsimd.tensor_tensor(out=res[g][:, k, :], in0=res[g][:, k, :], in1=gamma_sb[:], op=ALU.mult)
+                nc.gpsimd.tensor_scalar(
+                    out=res[g][:, k, :],
+                    in0=res[g][:, k, :],
+                    scalar1=rstd[g][:, k : k + 1],
+                    scalar2=0.0,
+                    op0=ALU.mult,
+                    op1=ALU.add,
+                )
                 nc.gpsimd.tensor_tensor(out=res[g][:, k, :], in0=res[g][:, k, :], in1=beta_sb[:], op=ALU.add)
                 store(g, k)
 
@@ -345,8 +338,6 @@ def tile_densegatlayer_pb_kernel(
         nc.vector.tensor_scalar_mul(out=neg_c_mean[:], in0=c_sum[:], scalar1=-1.0 / FEAT)
         gamma_ps = repeat_vector(0, "const_a")
         beta_ps = repeat_vector(1, "const_b")
-        gamma_sb = consts.tile([P, FEAT], F32, name="gamma_sb")
-        nc.scalar.copy(out=gamma_sb[:], in_=gamma_ps[:])
         beta_sb = consts.tile([P, FEAT], F32, name="beta_sb")
         nc.scalar.copy(out=beta_sb[:], in_=beta_ps[:])
 
@@ -378,6 +369,5 @@ def tile_densegatlayer_pb_kernel(
             if in_range(i - 1):
                 centre_and_gain(i - 1)
                 deviation(i - 1)
-                standardise_handed_over(i - 1)
             if in_range(i - 2):
                 normalise(i - 2)

@@ -272,8 +272,17 @@ def tile_densegatlayer_pb_kernel(
         mask(0)
         transpose(0)
         unload(0)
+
+        def repeat_vector(v, bank_name):
+            bank = psum_const.tile([P, FEAT], F32, name=bank_name)
+            nc.tensor.matmul(out=bank[:], lhsT=ones[:], rhs=vec_rows[:, v, :], start=True, stop=True)
+            return bank
+
+        bias_ps = repeat_vector(2, "const_a")
+        bias_all = consts.tile([P, FEAT], F32, name="bias_all")
+        nc.scalar.copy(out=bias_all[:], in_=bias_ps[:])
+        regroup_w(0, nc.scalar.copy)
         mask(1)
-        transpose(1)
         regroup_w(2, nc.vector.tensor_copy)
         node_grouped = consts.tile([P, GRAPHS, NODES, PACK], BF16, name="node_grouped", align_bytes=64)
         nc.vector.tensor_copy(
@@ -307,17 +316,8 @@ def tile_densegatlayer_pb_kernel(
             scales=node_scales[:],
             in_=node_grouped[:].rearrange("p b n t -> p (b n t)"),
         )
-        regroup_w(0, nc.scalar.copy)
         quantise_w(0)
 
-        def repeat_vector(v, bank_name):
-            bank = psum_const.tile([P, FEAT], F32, name=bank_name)
-            nc.tensor.matmul(out=bank[:], lhsT=ones[:], rhs=vec_rows[:, v, :], start=True, stop=True)
-            return bank
-
-        bias_ps = repeat_vector(2, "const_a")
-        bias_all = consts.tile([P, FEAT], F32, name="bias_all")
-        nc.scalar.copy(out=bias_all[:], in_=bias_ps[:])
         row_ps = psum_const.tile([P, FEAT], F32, name="const_b")
         nc.tensor.matmul_mx(
             out=row_ps[:],
@@ -328,6 +328,8 @@ def tile_densegatlayer_pb_kernel(
             start=True,
             stop=True,
         )
+        transpose(1)
+        unload(1)
         repeat_codes(1, 2)
         c = consts.tile([P, FEAT], F32, name="c")
         c_sum = consts.tile([P, 1], F32, name="c_sum")
@@ -350,15 +352,12 @@ def tile_densegatlayer_pb_kernel(
         for i in range(N_GROUPS + 2):
             if in_range(i + LOADS_AHEAD):
                 load(i + LOADS_AHEAD)
-            if in_range(i + 1):
-                unload(i + 1)
             if in_range(i - 2):
                 normalise_handed_over(i - 2)
             if in_range(i):
                 residual(i)
             if in_range(i + 1):
                 quantise(i + 1)
-                products(i + 1)
             if i in repeated_in_round:
                 repeat_codes(*repeated_in_round[i])
             if in_range(i - 1):
@@ -366,6 +365,9 @@ def tile_densegatlayer_pb_kernel(
             if in_range(i + 2):
                 mask(i + 2)
                 transpose(i + 2)
+                unload(i + 2)
+            if in_range(i + 1):
+                products(i + 1)
             if in_range(i - 1):
                 centre_and_gain(i - 1)
                 deviation(i - 1)

@@ -12,15 +12,19 @@ ACT = mybir.ActivationFunctionType
 
 P = 128
 PACK = 4
+HALVES = 2
 GRAPHS = 2
 NODES = 64
 FEAT = 512
+BLOCKS = FEAT // P
 GROUP = 4
 N_GROUPS = NODES // GROUP
 PAIR = 2
 REP = 4
-HANDED_OVER = 1
-LOADS_AHEAD = 4
+LOADS_AHEAD = 5
+HEAD_MASKS = 1
+SCALED_BY_GPSIMD = (2,)
+SHAPED_BY_GPSIMD = (3,)
 LN_EPS = 1e-5
 
 FLOPS = 2 * (GRAPHS * NODES * NODES + 2 * GRAPHS * NODES) * FEAT * FEAT
@@ -42,11 +46,12 @@ def tile_densegatlayer_pb_kernel(
         tc.tile_pool(name="small", bufs=4) as small,
         tc.psum_pool(name="psum_const", bufs=1) as psum_const,
         tc.psum_pool(name="psum_t", bufs=2) as psum_t,
-        tc.psum_pool(name="psum_acc", bufs=GROUP) as psum_acc,
+        tc.psum_pool(name="psum_prod", bufs=2) as psum_prod,
+        tc.psum_pool(name="psum_acc", bufs=3) as psum_acc,
         tc.manual_schedule(),
     ):
-        emb_sb, xe_bf, xt, grouped, codes, scales = {}, {}, {}, {}, {}, {}
-        acc, y, row_sum, neg_mean, rstd, res = {}, {}, {}, {}, {}, {}
+        emb_sb, xe_bf, xt, grouped, codes, scales, prod_t = {}, {}, {}, {}, {}, {}, {}
+        acc, y, row_sum, neg_mean, sq_sum, rstd, res = {}, {}, {}, {}, {}, {}, {}
 
         def load(g):
             emb_sb[g] = emb_pool.tile([P, GROUP, FEAT], BF16, name="emb_sb")
@@ -62,23 +67,24 @@ def tile_densegatlayer_pb_kernel(
             )
         node_sb = consts.tile([P, FEAT], BF16, name="node_sb")
         nc.sync.dma_start(out=node_sb[:], in_=new_node.rearrange("b n f -> (b n) f"))
-        load(0)
         w_raw = {}
         for blk in (2, 1, 0):
             w_raw[blk] = w_stage.tile([P, PACK, FEAT], BF16, name="w_raw")
             nc.sync.dma_start(
-                out=w_raw[blk][:],
-                in_=Wedge[blk * FEAT : (blk + 1) * FEAT, :].rearrange("(t p) n -> p t n", p=P),
+                out=w_raw[blk][:].rearrange("p (u e) n -> p u (e n)", u=HALVES),
+                in_=Wedge[blk * FEAT : (blk + 1) * FEAT, :].rearrange("(u p e) n -> p u (e n)", u=HALVES, p=P),
             )
-        for g in range(1, LOADS_AHEAD):
-            load(g)
-
-        ident = consts.tile([P, P], BF16, name="ident")
-        make_identity(nc, ident[:])
+            if blk == 2:
+                load(0)
         vec_rows = consts.tile([P, 3, FEAT], BF16, name="vec_rows")
         nc.vector.memset(vec_rows[:], 0.0)
         for v, vec in enumerate((gamma_e, beta_e, bedge)):
-            nc.gpsimd.dma_start(out=vec_rows[0:1, v, :], in_=vec.rearrange("(o f) -> o f", o=1))
+            nc.sync.dma_start(out=vec_rows[0:1, v, :], in_=vec.rearrange("(o f) -> o f", o=1))
+        for g in range(1, LOADS_AHEAD):
+            load(g)
+
+        ident = consts.tile([P, P], F32, name="ident")
+        make_identity(nc, ident[:])
         ones = consts.tile([P, P], BF16, name="ones")
         nc.vector.memset(ones[:], 1.0)
         eps = consts.tile([P, 1], F32, name="eps")
@@ -91,115 +97,133 @@ def tile_densegatlayer_pb_kernel(
         e_mask = consts.tile([P, NODES], F32, name="e_mask")
         nc.vector.tensor_scalar_mul(out=e_mask[:], in0=mask_row[:], scalar1=mask_col[:, 0:1])
 
+        def scaled_by_gpsimd(g):
+            return SCALED_BY_GPSIMD if g < N_GROUPS - 1 else ()
+
+        def shaped_by_gpsimd(g):
+            return SHAPED_BY_GPSIMD if g < N_GROUPS - 1 else ()
+
         def mask(g):
             xe_bf[g] = front.tile([P, GROUP, FEAT], BF16, name="xe_bf")
             for k in range(GROUP):
                 j = g * GROUP + k
-                nc.scalar.activation(
-                    out=xe_bf[g][:, k, :], in_=emb_sb[g][:, k, :], func=ACT.Copy, scale=e_mask[:, j : j + 1]
-                )
+                if g < HEAD_MASKS:
+                    nc.scalar.activation(
+                        out=xe_bf[g][:, k, :], in_=emb_sb[g][:, k, :], func=ACT.Copy, scale=e_mask[:, j : j + 1]
+                    )
+                else:
+                    nc.vector.tensor_scalar_mul(
+                        out=xe_bf[g][:, k, :], in0=emb_sb[g][:, k, :], scalar1=e_mask[:, j : j + 1]
+                    )
 
         def transpose(g):
             xt[g] = []
             for h in range(GROUP // PAIR):
-                bank = psum_t.tile([P, PAIR, PACK, P], BF16, name="xt")
+                bank = psum_t.tile([P, PAIR, HALVES, P], F32, name="xt")
                 for k in range(PAIR):
-                    for t in range(PACK):
-                        nc.tensor.transpose(
-                            bank[:, k, t, :], xe_bf[g][:, h * PAIR + k, t * P : (t + 1) * P], ident[:]
-                        )
+                    words = xe_bf[g][:, h * PAIR + k, :].bitcast(F32)
+                    for u in range(HALVES):
+                        nc.tensor.transpose(bank[:, k, u, :], words[:, u * P : (u + 1) * P], ident[:])
                 xt[g].append(bank)
 
-        def unload(g):
-            grouped[g] = front.tile([P, GROUP, P, PACK], BF16, name="grouped", align_bytes=64)
-            for h in range(GROUP // PAIR):
-                nc.scalar.copy(
-                    out=grouped[g][:, h * PAIR : (h + 1) * PAIR, :, :],
-                    in_=xt[g][h][:].rearrange("p k t r -> p k r t"),
-                )
+        def unload(g, h):
+            if h == 0:
+                grouped[g] = front.tile([P, GROUP, P, PACK], BF16, name="grouped", align_bytes=64)
+            nc.scalar.copy(
+                out=grouped[g][:, h * PAIR : (h + 1) * PAIR, :, :].bitcast(F32),
+                in_=xt[g][h][:].rearrange("p k u r -> p k r u"),
+            )
 
         def quantise(g):
-            codes[g] = front.tile([P, GROUP, P], U32, name="codes", align_bytes=64)
-            scales[g] = front.tile([P, GROUP, P], U8, name="scales", align_bytes=64)
+            codes[g] = front.tile([P, GROUP * P], U32, name="codes", align_bytes=64)
+            scales[g] = front.tile([P, GROUP * P], U8, name="scales", align_bytes=64)
             nc.vector.quantize_mx(
-                out=codes[g][:].rearrange("p k r -> p (k r)").bitcast(FP8X4),
-                scales=scales[g][:].rearrange("p k r -> p (k r)"),
+                out=codes[g][:].bitcast(FP8X4),
+                scales=scales[g][:],
                 in_=grouped[g][:].rearrange("p k r t -> p (k r t)"),
             )
 
-        def products(g):
-            acc[g] = []
-            for k in range(GROUP):
-                bank = psum_acc.tile([P, FEAT], F32, name="acc")
+        def products(g, f):
+            features = slice(f * P, (f + 1) * P)
+            rows = slice(g * GROUP * P, (g + 1) * GROUP * P)
+            bank = psum_prod.tile([P, GROUP * P], F32, name="prod")
+            operands = (
+                (2, codes[g][:], scales[g][:]),
+                (1, col_codes[:, rows], col_scales[:, rows]),
+                (0, row_codes[:], row_scales[:]),
+            )
+            for n, (blk, row_words, row_bytes) in enumerate(operands):
                 nc.tensor.matmul_mx(
                     out=bank[:],
-                    lhsT=codes[g][:, k, :].bitcast(FP8X4),
-                    lhsT_scale=scales[g][:, k, :],
-                    rhs=w_codes[:, 2, :].bitcast(FP8X4),
-                    rhs_scale=w_scales[:, 2, :],
-                    start=True,
-                    stop=False,
+                    lhsT=w_codes[:, blk, features].bitcast(FP8X4),
+                    lhsT_scale=w_scales[:, blk, features],
+                    rhs=row_words.bitcast(FP8X4),
+                    rhs_scale=row_bytes,
+                    start=n == 0,
+                    stop=n == len(operands) - 1,
                 )
-                nc.tensor.matmul_mx(
-                    out=bank[:],
-                    lhsT=col_codes[:, g * GROUP + k, :].bitcast(FP8X4),
-                    lhsT_scale=col_scales[:, g * GROUP + k, :],
-                    rhs=w_codes[:, 1, :].bitcast(FP8X4),
-                    rhs_scale=w_scales[:, 1, :],
-                    start=False,
-                    stop=True,
-                )
-                acc[g].append(bank)
+            if f == 0:
+                prod_t[g] = front.tile([P, BLOCKS, GROUP, P], F32, name="prod_t")
+            nc.scalar.activation(
+                out=prod_t[g][:, f, :, :].rearrange("p k r -> p (k r)"),
+                in_=bank[:],
+                func=ACT.Identity,
+                bias=bias_col[:, f : f + 1],
+                scale=1.0,
+            )
 
-        def residual(g):
-            y[g] = back.tile([P, GROUP, FEAT], F32, name="y")
-            row_sum[g] = small.tile([P, GROUP], F32, name="row_sum")
-            for k in reversed(range(GROUP)):
-                j = g * GROUP + k
-                nc.vector.scalar_tensor_tensor(
-                    out=y[g][:, k, :],
-                    in0=emb_sb[g][:, k, :],
-                    scalar=e_mask[:, j : j + 1],
-                    in1=acc[g][k][:],
-                    op0=ALU.mult,
-                    op1=ALU.add,
-                    accum_out=row_sum[g][:, k : k + 1],
-                )
-            nc.gpsimd.tensor_tensor(
-                out=y[g][:], in0=y[g][:], in1=c[:].unsqueeze(1).to_broadcast([P, GROUP, FEAT]), op=ALU.add
+        def turn_back(g, k):
+            acc[g, k] = psum_acc.tile([P, FEAT], F32, name="acc")
+            for f in range(BLOCKS):
+                nc.tensor.transpose(acc[g, k][:, f * P : (f + 1) * P], prod_t[g][:, f, k, :], ident[:])
+
+        def residual(g, k):
+            if k == 0:
+                y[g] = back.tile([P, GROUP, FEAT], F32, name="y")
+                row_sum[g] = small.tile([P, GROUP], F32, name="row_sum")
+            j = g * GROUP + k
+            nc.vector.scalar_tensor_tensor(
+                out=y[g][:, k, :],
+                in0=emb_sb[g][:, k, :],
+                scalar=e_mask[:, j : j + 1],
+                in1=acc[g, k][:],
+                op0=ALU.mult,
+                op1=ALU.add,
+                accum_out=row_sum[g][:, k : k + 1],
             )
 
         def mean(g):
             neg_mean[g] = small.tile([P, GROUP], F32, name="neg_mean")
+            nc.scalar.activation(out=neg_mean[g][:], in_=row_sum[g][:], func=ACT.Copy, scale=-1.0 / FEAT)
+
+        def deviation(g, k):
+            if k == 0:
+                sq_sum[g] = small.tile([P, GROUP], F32, name="sq_sum")
+            squares = small.tile([P, FEAT], BF16, name="squares")
             nc.scalar.activation(
-                out=neg_mean[g][:], in_=row_sum[g][:], func=ACT.Identity, bias=neg_c_mean[:, 0:1], scale=-1.0 / FEAT
+                out=squares[:],
+                in_=y[g][:, k, :],
+                func=ACT.Square,
+                bias=neg_mean[g][:, k : k + 1],
+                scale=1.0,
+                accum_out=sq_sum[g][:, k : k + 1],
             )
 
-        def deviation(g):
-            sq_sum = small.tile([P, GROUP], F32, name="sq_sum")
-            for k in range(GROUP):
-                squares = small.tile([P, FEAT], BF16, name="squares")
-                nc.scalar.activation(
-                    out=squares[:],
-                    in_=y[g][:, k, :],
-                    func=ACT.Square,
-                    bias=neg_mean[g][:, k : k + 1],
-                    scale=1.0,
-                    accum_out=sq_sum[:, k : k + 1],
-                )
+        def finish_statistics(g):
             rstd[g] = small.tile([P, GROUP], F32, name="rstd")
             nc.scalar.activation(
-                out=rstd[g][:], in_=sq_sum[:], func=ACT.Abs_reciprocal_sqrt, bias=eps[:, 0:1], scale=1.0 / FEAT
+                out=rstd[g][:], in_=sq_sum[g][:], func=ACT.Abs_reciprocal_sqrt, bias=eps[:, 0:1], scale=1.0 / FEAT
             )
 
-        def centre_and_gain(g):
-            res[g] = back.tile([P, GROUP, FEAT], F32, name="res")
-            for k in range(GROUP):
+        def centre_and_gain(g, k):
+            if k == 0:
+                res[g] = back.tile([P, GROUP, FEAT], F32, name="res")
+            if k not in shaped_by_gpsimd(g):
                 nc.vector.scalar_tensor_tensor(
                     out=res[g][:, k, :],
                     in0=y[g][:, k, :],
                     scalar=neg_mean[g][:, k : k + 1],
-                    in1=gamma_ps[:],
+                    in1=gamma_beta_ps[:, 0, :],
                     op0=ALU.add,
                     op1=ALU.mult,
                 )
@@ -207,8 +231,29 @@ def tile_densegatlayer_pb_kernel(
         def store(g, k):
             nc.sync.dma_start(out=out_rows[:, g * GROUP + k, :], in_=res[g][:, k, :])
 
+        def normalise(g, k):
+            if k not in shaped_by_gpsimd(g) + scaled_by_gpsimd(g):
+                nc.vector.scalar_tensor_tensor(
+                    out=res[g][:, k, :],
+                    in0=res[g][:, k, :],
+                    scalar=rstd[g][:, k : k + 1],
+                    in1=gamma_beta_ps[:, 1, :],
+                    op0=ALU.mult,
+                    op1=ALU.add,
+                )
+                store(g, k)
+
         def normalise_handed_over(g):
-            for k in range(HANDED_OVER):
+            for k in shaped_by_gpsimd(g):
+                nc.gpsimd.tensor_scalar(
+                    out=res[g][:, k, :],
+                    in0=y[g][:, k, :],
+                    scalar1=neg_mean[g][:, k : k + 1],
+                    scalar2=rstd[g][:, k : k + 1],
+                    op0=ALU.add,
+                    op1=ALU.mult,
+                )
+            for k in scaled_by_gpsimd(g):
                 nc.gpsimd.tensor_scalar(
                     out=res[g][:, k, :],
                     in0=res[g][:, k, :],
@@ -217,20 +262,15 @@ def tile_densegatlayer_pb_kernel(
                     op0=ALU.mult,
                     op1=ALU.add,
                 )
+            for k in shaped_by_gpsimd(g):
+                nc.gpsimd.tensor_tensor(out=res[g][:, k, :], in0=res[g][:, k, :], in1=gamma_sb[:], op=ALU.mult)
+            for k in scaled_by_gpsimd(g) + shaped_by_gpsimd(g):
                 nc.gpsimd.tensor_tensor(out=res[g][:, k, :], in0=res[g][:, k, :], in1=beta_sb[:], op=ALU.add)
                 store(g, k)
 
-        def normalise(g):
-            for k in range(HANDED_OVER, GROUP):
-                nc.vector.scalar_tensor_tensor(
-                    out=res[g][:, k, :],
-                    in0=res[g][:, k, :],
-                    scalar=rstd[g][:, k : k + 1],
-                    in1=beta_ps[:],
-                    op0=ALU.mult,
-                    op1=ALU.add,
-                )
-                store(g, k)
+        def take_turn(g):
+            turn = small.tile([P, 1], U32, name="turn")
+            nc.gpsimd.tensor_copy(out=turn[:], in_=codes[g][:, 0:1])
 
         w_codes = consts.tile([P, 3, FEAT], U32, name="w_codes", align_bytes=64)
         w_scales = consts.tile([P, 3, FEAT], U8, name="w_scales", align_bytes=64)
@@ -250,101 +290,90 @@ def tile_densegatlayer_pb_kernel(
                 in_=w_grouped[blk][:].rearrange("p n t -> p (n t)"),
             )
 
-        col4_codes = consts.tile([P, NODES * GRAPHS, REP], U32, name="col4_codes", align_bytes=64)
-        col4_scales = consts.tile([P, NODES * GRAPHS, REP], U8, name="col4_scales", align_bytes=64)
-        nc.vector.memset(col4_scales[:].bitcast(I32), 0)
-        col_codes = consts.tile([P, NODES, P], U32, name="col_codes", align_bytes=64)
-        col_scales = consts.tile([P, NODES, P], U8, name="col_scales", align_bytes=64)
+        node_codes = consts.tile([P, P], U32, name="node_codes", align_bytes=64)
+        node_scales = consts.tile([P, P], U8, name="node_scales", align_bytes=64)
+        nc.vector.memset(node_scales[:].bitcast(I32), 0)
+        scales4 = consts.tile([P, NODES * GRAPHS, REP], U8, name="scales4", align_bytes=64)
+        col_codes = consts.tile([P, NODES * P], U32, name="col_codes", align_bytes=64)
+        col_scales = consts.tile([P, NODES * P], U8, name="col_scales", align_bytes=64)
+        row_codes = consts.tile([P, GROUP * P], U32, name="row_codes", align_bytes=64)
+        row_scales = consts.tile([P, GROUP * P], U8, name="row_scales", align_bytes=64)
 
         def repeat_codes(g0, g1):
             j0, j1 = g0 * GROUP, g1 * GROUP
             nc.vector.tensor_copy(
-                out=col_codes[:, j0:j1, :].bitcast(I32).rearrange("p j (b s r) -> p (j b) s r", b=GRAPHS, r=REP),
-                in_=col4_codes[:, j0 * GRAPHS : j1 * GRAPHS, :]
+                out=col_codes[:, j0 * P : j1 * P].bitcast(I32).rearrange("p (j b s) -> p j b s", b=GRAPHS, s=NODES),
+                in_=node_codes[:]
                 .bitcast(I32)
-                .unsqueeze(2)
-                .to_broadcast([P, (j1 - j0) * GRAPHS, NODES // REP, REP]),
+                .rearrange("p (b j) -> p j b", b=GRAPHS)[:, j0:j1, :]
+                .unsqueeze(3)
+                .to_broadcast([P, j1 - j0, GRAPHS, NODES]),
             )
 
-        node_t = psum_t.tile([P, PAIR, PACK, P], BF16, name="xt")
-        for t in range(PACK):
-            nc.tensor.transpose(node_t[:, 0, t, :], node_sb[:, t * P : (t + 1) * P], ident[:])
+        node_t = psum_t.tile([P, PAIR, HALVES, P], F32, name="xt")
+        for u in range(HALVES):
+            nc.tensor.transpose(node_t[:, 0, u, :], node_sb[:].bitcast(F32)[:, u * P : (u + 1) * P], ident[:])
         mask(0)
         transpose(0)
-        unload(0)
-
-        def repeat_vector(v, bank_name):
-            bank = psum_const.tile([P, FEAT], F32, name=bank_name)
-            nc.tensor.matmul(out=bank[:], lhsT=ones[:], rhs=vec_rows[:, v, :], start=True, stop=True)
-            return bank
-
-        bias_ps = repeat_vector(2, "const_a")
-        bias_all = consts.tile([P, FEAT], F32, name="bias_all")
-        nc.scalar.copy(out=bias_all[:], in_=bias_ps[:])
+        for h in range(GROUP // PAIR):
+            unload(0, h)
         regroup_w(0, nc.scalar.copy)
-        mask(1)
+        bias_ps = psum_acc.tile([P, BLOCKS, 2], F32, name="acc")
+        for f in range(BLOCKS):
+            nc.tensor.matmul(
+                out=bias_ps[:, f, :], lhsT=vec_rows[:, 2, f * P : (f + 1) * P], rhs=ones[:, 0:2], start=True, stop=True
+            )
+        bias_col = consts.tile([P, BLOCKS], F32, name="bias_col")
+        nc.scalar.copy(out=bias_col[:], in_=bias_ps[:, :, 0])
         regroup_w(2, nc.vector.tensor_copy)
         node_grouped = consts.tile([P, GRAPHS, NODES, PACK], BF16, name="node_grouped", align_bytes=64)
         nc.vector.tensor_copy(
-            out=node_grouped[:], in_=node_t[:, 0, :, :].rearrange("p t (b n) -> p b n t", b=GRAPHS)
+            out=node_grouped[:].bitcast(F32), in_=node_t[:, 0, :, :].rearrange("p u (b n) -> p b n u", b=GRAPHS)
         )
         quantise_w(2)
-        col_grouped = consts.tile([P, NODES, GRAPHS, REP, PACK], BF16, name="col_grouped", align_bytes=64)
-        for b in range(GRAPHS):
-            nc.vector.tensor_copy(
-                out=col_grouped[:, :, b, :, :],
-                in_=node_grouped[:, b, :, :].unsqueeze(2).to_broadcast([P, NODES, REP, PACK]),
-            )
-        regroup_w(1, nc.vector.tensor_copy)
-        nc.vector.quantize_mx(
-            out=col4_codes[:].rearrange("p a r -> p (a r)").bitcast(FP8X4),
-            scales=col4_scales[:].rearrange("p a r -> p (a r)"),
-            in_=col_grouped[:].rearrange("p j b r t -> p (j b r t)"),
-        )
-        quantise_w(1)
-        nc.vector.tensor_copy(
-            out=col_scales[:].bitcast(I32).rearrange("p j (b s) -> p (j b) s", b=GRAPHS),
-            in_=col4_scales[:].bitcast(I32).to_broadcast([P, NODES * GRAPHS, NODES // REP]),
-        )
-        repeat_codes(0, 1)
-        quantise(0)
-        products(0)
-        node_codes = consts.tile([P, P], U32, name="node_codes", align_bytes=64)
-        node_scales = consts.tile([P, P], U8, name="node_scales", align_bytes=64)
         nc.vector.quantize_mx(
             out=node_codes[:].bitcast(FP8X4),
             scales=node_scales[:],
             in_=node_grouped[:].rearrange("p b n t -> p (b n t)"),
         )
-        quantise_w(0)
-
-        row_ps = psum_const.tile([P, FEAT], F32, name="const_b")
-        nc.tensor.matmul_mx(
-            out=row_ps[:],
-            lhsT=node_codes[:].bitcast(FP8X4),
-            lhsT_scale=node_scales[:],
-            rhs=w_codes[:, 0, :].bitcast(FP8X4),
-            rhs_scale=w_scales[:, 0, :],
-            start=True,
-            stop=True,
-        )
+        regroup_w(1, nc.vector.tensor_copy)
+        for r in range(REP):
+            nc.vector.tensor_copy(
+                out=scales4[:].rearrange("p (j b) r -> p b j r", b=GRAPHS)[:, :, :, r],
+                in_=node_scales[:].rearrange("p (b j) -> p b j", b=GRAPHS),
+            )
+        mask(1)
         transpose(1)
-        unload(1)
-        repeat_codes(1, 2)
-        c = consts.tile([P, FEAT], F32, name="c")
-        c_sum = consts.tile([P, 1], F32, name="c_sum")
-        nc.vector.scalar_tensor_tensor(
-            out=c[:], in0=row_ps[:], scalar=1.0, in1=bias_all[:], op0=ALU.mult, op1=ALU.add, accum_out=c_sum[:]
+        for h in range(GROUP // PAIR):
+            unload(1, h)
+        quantise_w(1)
+        nc.vector.tensor_copy(
+            out=col_scales[:].bitcast(I32).rearrange("p (a s) -> p a s", a=NODES * GRAPHS),
+            in_=scales4[:].bitcast(I32).to_broadcast([P, NODES * GRAPHS, NODES // REP]),
         )
-        neg_c_mean = consts.tile([P, 1], F32, name="neg_c_mean")
-        nc.vector.tensor_scalar_mul(out=neg_c_mean[:], in0=c_sum[:], scalar1=-1.0 / FEAT)
-        gamma_ps = repeat_vector(0, "const_a")
-        beta_ps = repeat_vector(1, "const_b")
+        repeat_codes(0, 1)
+        quantise(0)
+        for out_tile, in_tile in ((row_codes, node_codes), (row_scales, node_scales)):
+            words = in_tile[:].bitcast(I32)
+            nc.vector.tensor_copy(
+                out=out_tile[:].bitcast(I32).rearrange("p (k r) -> p k r", k=GROUP),
+                in_=words.unsqueeze(1).to_broadcast([P, GROUP, words.shape[1]]),
+            )
+        quantise_w(0)
+        for f in range(BLOCKS):
+            products(0, f)
+        repeat_codes(1, 2)
+        quantise(1)
+        mask(2)
+        transpose(2)
+        gamma_beta_ps = psum_const.tile([P, 2, FEAT], BF16, name="gamma_beta_ps")
+        for v in range(2):
+            nc.tensor.matmul(out=gamma_beta_ps[:, v, :], lhsT=ones[:], rhs=vec_rows[:, v, :], start=True, stop=True)
+        gamma_sb = consts.tile([P, FEAT], F32, name="gamma_sb")
+        nc.scalar.copy(out=gamma_sb[:], in_=gamma_beta_ps[:, 0, :])
         beta_sb = consts.tile([P, FEAT], F32, name="beta_sb")
-        nc.scalar.copy(out=beta_sb[:], in_=beta_ps[:])
-
-        half = 2 + (N_GROUPS - 2) // 2
-        repeated_in_round = {0: (2, half), 1: (half, N_GROUPS)}
+        nc.scalar.copy(out=beta_sb[:], in_=gamma_beta_ps[:, 1, :])
+        repeat_codes(2, N_GROUPS)
 
         def in_range(g):
             return 0 <= g < N_GROUPS
@@ -352,24 +381,31 @@ def tile_densegatlayer_pb_kernel(
         for i in range(N_GROUPS + 2):
             if in_range(i + LOADS_AHEAD):
                 load(i + LOADS_AHEAD)
-            if in_range(i - 2):
-                normalise_handed_over(i - 2)
-            if in_range(i):
-                residual(i)
-            if in_range(i + 1):
-                quantise(i + 1)
-            if i in repeated_in_round:
-                repeat_codes(*repeated_in_round[i])
             if in_range(i - 1):
                 mean(i - 1)
-            if in_range(i + 2):
-                mask(i + 2)
-                transpose(i + 2)
-                unload(i + 2)
-            if in_range(i + 1):
-                products(i + 1)
-            if in_range(i - 1):
-                centre_and_gain(i - 1)
-                deviation(i - 1)
             if in_range(i - 2):
-                normalise(i - 2)
+                finish_statistics(i - 2)
+            for k in range(GROUP):
+                if in_range(i):
+                    turn_back(i, k)
+                    residual(i, k)
+                if in_range(i + 2) and k < GROUP // PAIR:
+                    unload(i + 2, k)
+                if in_range(i + 1):
+                    products(i + 1, k)
+                if in_range(i - 1):
+                    centre_and_gain(i - 1, k)
+                    deviation(i - 1, k)
+                if in_range(i - 2):
+                    normalise(i - 2, k)
+                if k == 2:
+                    if in_range(i + 3):
+                        mask(i + 3)
+                    if in_range(i + 2):
+                        quantise(i + 2)
+            if in_range(i + 3):
+                transpose(i + 3)
+            if in_range(i - 2):
+                if in_range(i + 2):
+                    take_turn(i + 2)
+                normalise_handed_over(i - 2)

@@ -42,7 +42,8 @@ def tile_densegatlayer_pb_kernel(
         tc.tile_pool(name="w_stage", bufs=3) as w_stage,
         tc.tile_pool(name="emb_pool", bufs=LOADS_AHEAD + 2) as emb_pool,
         tc.tile_pool(name="front", bufs=2) as front,
-        tc.tile_pool(name="back", bufs=3) as back,
+        tc.tile_pool(name="y_pool", bufs=4) as y_pool,
+        tc.tile_pool(name="back", bufs=4) as back,
         tc.tile_pool(name="small", bufs=4) as small,
         tc.psum_pool(name="psum_const", bufs=1) as psum_const,
         tc.psum_pool(name="psum_t", bufs=2) as psum_t,
@@ -179,7 +180,7 @@ def tile_densegatlayer_pb_kernel(
 
         def residual(g, k):
             if k == 0:
-                y[g] = back.tile([P, GROUP, FEAT], F32, name="y")
+                y[g] = y_pool.tile([P, GROUP, FEAT], F32, name="y")
                 row_sum[g] = small.tile([P, GROUP], F32, name="row_sum")
             j = g * GROUP + k
             nc.vector.scalar_tensor_tensor(
@@ -299,8 +300,14 @@ def tile_densegatlayer_pb_kernel(
         row_codes = consts.tile([P, GROUP * P], U32, name="row_codes", align_bytes=64)
         row_scales = consts.tile([P, GROUP * P], U8, name="row_scales", align_bytes=64)
 
-        def repeat_codes(g0, g1):
+        def repeat_nodes(g0, g1):
             j0, j1 = g0 * GROUP, g1 * GROUP
+            nc.vector.tensor_copy(
+                out=col_scales[:, j0 * P : j1 * P].bitcast(I32).rearrange("p (a s) -> p a s", a=(j1 - j0) * GRAPHS),
+                in_=scales4[:, j0 * GRAPHS : j1 * GRAPHS, :]
+                .bitcast(I32)
+                .to_broadcast([P, (j1 - j0) * GRAPHS, NODES // REP]),
+            )
             nc.vector.tensor_copy(
                 out=col_codes[:, j0 * P : j1 * P].bitcast(I32).rearrange("p (j b s) -> p j b s", b=GRAPHS, s=NODES),
                 in_=node_codes[:]
@@ -342,17 +349,13 @@ def tile_densegatlayer_pb_kernel(
                 out=scales4[:].rearrange("p (j b) r -> p b j r", b=GRAPHS)[:, :, :, r],
                 in_=node_scales[:].rearrange("p (b j) -> p b j", b=GRAPHS),
             )
+        quantise(0)
         mask(1)
         transpose(1)
         for h in range(GROUP // PAIR):
             unload(1, h)
         quantise_w(1)
-        nc.vector.tensor_copy(
-            out=col_scales[:].bitcast(I32).rearrange("p (a s) -> p a s", a=NODES * GRAPHS),
-            in_=scales4[:].bitcast(I32).to_broadcast([P, NODES * GRAPHS, NODES // REP]),
-        )
-        repeat_codes(0, 1)
-        quantise(0)
+        repeat_nodes(0, 1)
         for out_tile, in_tile in ((row_codes, node_codes), (row_scales, node_scales)):
             words = in_tile[:].bitcast(I32)
             nc.vector.tensor_copy(
@@ -362,9 +365,10 @@ def tile_densegatlayer_pb_kernel(
         quantise_w(0)
         for f in range(BLOCKS):
             products(0, f)
-        repeat_codes(1, 2)
+        repeat_nodes(1, 2)
         quantise(1)
         mask(2)
+        turn_back(0, 0)
         transpose(2)
         gamma_beta_ps = psum_const.tile([P, 2, FEAT], BF16, name="gamma_beta_ps")
         for v in range(2):
@@ -373,7 +377,7 @@ def tile_densegatlayer_pb_kernel(
         nc.scalar.copy(out=gamma_sb[:], in_=gamma_beta_ps[:, 0, :])
         beta_sb = consts.tile([P, FEAT], F32, name="beta_sb")
         nc.scalar.copy(out=beta_sb[:], in_=gamma_beta_ps[:, 1, :])
-        repeat_codes(2, N_GROUPS)
+        repeat_nodes(2, 7)
 
         def in_range(g):
             return 0 <= g < N_GROUPS
@@ -387,7 +391,8 @@ def tile_densegatlayer_pb_kernel(
                 finish_statistics(i - 2)
             for k in range(GROUP):
                 if in_range(i):
-                    turn_back(i, k)
+                    if k + 1 < GROUP:
+                        turn_back(i, k + 1)
                     residual(i, k)
                 if in_range(i + 2) and k < GROUP // PAIR:
                     unload(i + 2, k)
@@ -398,13 +403,17 @@ def tile_densegatlayer_pb_kernel(
                     deviation(i - 1, k)
                 if in_range(i - 2):
                     normalise(i - 2, k)
-                if k == 2:
+                if i == 0 and k < 3:
+                    repeat_nodes(7 + 3 * k, min(10 + 3 * k, N_GROUPS))
+                if k == 1:
                     if in_range(i + 3):
                         mask(i + 3)
                     if in_range(i + 2):
                         quantise(i + 2)
             if in_range(i + 3):
                 transpose(i + 3)
+            if in_range(i + 1):
+                turn_back(i + 1, 0)
             if in_range(i - 2):
                 if in_range(i + 2):
                     take_turn(i + 2)

@@ -23,8 +23,8 @@ PAIR = 2
 REP = 4
 LOADS_AHEAD = 5
 HEAD_MASKS = 1
-SCALED_BY_GPSIMD = (2,)
-SHAPED_BY_GPSIMD = (3,)
+SCALED = 2
+SHAPED = 3
 LN_EPS = 1e-5
 
 FLOPS = 2 * (GRAPHS * NODES * NODES + 2 * GRAPHS * NODES) * FEAT * FEAT
@@ -98,11 +98,8 @@ def tile_densegatlayer_pb_kernel(
         e_mask = consts.tile([P, NODES], F32, name="e_mask")
         nc.vector.tensor_scalar_mul(out=e_mask[:], in0=mask_row[:], scalar1=mask_col[:, 0:1])
 
-        def scaled_by_gpsimd(g):
-            return SCALED_BY_GPSIMD if g < N_GROUPS - 1 else ()
-
-        def shaped_by_gpsimd(g):
-            return SHAPED_BY_GPSIMD if g < N_GROUPS - 1 else ()
+        def handed_over(g, k):
+            return k in (SCALED, SHAPED) and g < N_GROUPS - 1
 
         def mask(g):
             xe_bf[g] = front.tile([P, GROUP, FEAT], BF16, name="xe_bf")
@@ -219,7 +216,7 @@ def tile_densegatlayer_pb_kernel(
         def centre_and_gain(g, k):
             if k == 0:
                 res[g] = back.tile([P, GROUP, FEAT], F32, name="res")
-            if k not in shaped_by_gpsimd(g):
+            if not (handed_over(g, k) and k == SHAPED):
                 nc.vector.scalar_tensor_tensor(
                     out=res[g][:, k, :],
                     in0=y[g][:, k, :],
@@ -229,11 +226,12 @@ def tile_densegatlayer_pb_kernel(
                     op1=ALU.mult,
                 )
 
-        def store(g, k):
-            nc.sync.dma_start(out=out_rows[:, g * GROUP + k, :], in_=res[g][:, k, :])
+        def store(g, k, n=1):
+            j = g * GROUP + k
+            nc.sync.dma_start(out=out_rows[:, j : j + n, :], in_=res[g][:, k : k + n, :])
 
         def normalise(g, k):
-            if k not in shaped_by_gpsimd(g) + scaled_by_gpsimd(g):
+            if not handed_over(g, k):
                 nc.vector.scalar_tensor_tensor(
                     out=res[g][:, k, :],
                     in0=res[g][:, k, :],
@@ -245,29 +243,29 @@ def tile_densegatlayer_pb_kernel(
                 store(g, k)
 
         def normalise_handed_over(g):
-            for k in shaped_by_gpsimd(g):
-                nc.gpsimd.tensor_scalar(
-                    out=res[g][:, k, :],
-                    in0=y[g][:, k, :],
-                    scalar1=neg_mean[g][:, k : k + 1],
-                    scalar2=rstd[g][:, k : k + 1],
-                    op0=ALU.add,
-                    op1=ALU.mult,
-                )
-            for k in scaled_by_gpsimd(g):
-                nc.gpsimd.tensor_scalar(
-                    out=res[g][:, k, :],
-                    in0=res[g][:, k, :],
-                    scalar1=rstd[g][:, k : k + 1],
-                    scalar2=0.0,
-                    op0=ALU.mult,
-                    op1=ALU.add,
-                )
-            for k in shaped_by_gpsimd(g):
-                nc.gpsimd.tensor_tensor(out=res[g][:, k, :], in0=res[g][:, k, :], in1=gamma_sb[:], op=ALU.mult)
-            for k in scaled_by_gpsimd(g) + shaped_by_gpsimd(g):
-                nc.gpsimd.tensor_tensor(out=res[g][:, k, :], in0=res[g][:, k, :], in1=beta_sb[:], op=ALU.add)
-                store(g, k)
+            nc.gpsimd.tensor_scalar(
+                out=res[g][:, SHAPED, :],
+                in0=y[g][:, SHAPED, :],
+                scalar1=neg_mean[g][:, SHAPED : SHAPED + 1],
+                scalar2=rstd[g][:, SHAPED : SHAPED + 1],
+                op0=ALU.add,
+                op1=ALU.mult,
+            )
+            nc.gpsimd.tensor_scalar(
+                out=res[g][:, SCALED, :],
+                in0=res[g][:, SCALED, :],
+                scalar1=rstd[g][:, SCALED : SCALED + 1],
+                scalar2=0.0,
+                op0=ALU.mult,
+                op1=ALU.add,
+            )
+            nc.gpsimd.tensor_tensor(
+                out=res[g][:, SHAPED, :], in0=res[g][:, SHAPED, :], in1=gamma_sb[:], op=ALU.mult
+            )
+            both = res[g][:, SCALED : SHAPED + 1, :]
+            nc.gpsimd.tensor_tensor(
+                out=both, in0=both, in1=beta_sb[:].unsqueeze(1).to_broadcast([P, 2, FEAT]), op=ALU.add
+            )
 
         def take_turn(g):
             turn = small.tile([P, 1], U32, name="turn")
@@ -414,7 +412,9 @@ def tile_densegatlayer_pb_kernel(
                 transpose(i + 3)
             if in_range(i + 1):
                 turn_back(i + 1, 0)
-            if in_range(i - 2):
+            if in_range(i - 3) and i - 3 < N_GROUPS - 1:
+                store(i - 3, SCALED, 2)
+            if in_range(i - 2) and i - 2 < N_GROUPS - 1:
                 if in_range(i + 2):
                     take_turn(i + 2)
                 normalise_handed_over(i - 2)

@@ -22,7 +22,7 @@ N_GROUPS = NODES // GROUP
 PAIR = 2
 REP = 4
 LOADS_AHEAD = 5
-HEAD_MASKS = 1
+SCALAR_MASKS_FROM = 4
 SCALED = 2
 SHAPED = 3
 LN_EPS = 1e-5
@@ -41,6 +41,7 @@ def tile_densegatlayer_pb_kernel(
         tc.tile_pool(name="consts", bufs=1) as consts,
         tc.tile_pool(name="w_stage", bufs=3) as w_stage,
         tc.tile_pool(name="emb_pool", bufs=LOADS_AHEAD + 2) as emb_pool,
+        tc.tile_pool(name="xe_pool", bufs=3) as xe_pool,
         tc.tile_pool(name="front", bufs=2) as front,
         tc.tile_pool(name="y_pool", bufs=4) as y_pool,
         tc.tile_pool(name="back", bufs=4) as back,
@@ -52,7 +53,7 @@ def tile_densegatlayer_pb_kernel(
         tc.manual_schedule(),
     ):
         emb_sb, xe_bf, xt, grouped, codes, scales, prod_t = {}, {}, {}, {}, {}, {}, {}
-        acc, y, row_sum, neg_mean, sq_sum, rstd, res = {}, {}, {}, {}, {}, {}, {}
+        acc, y, row_sum, neg_mean, turn, sq_sum, rstd, res = {}, {}, {}, {}, {}, {}, {}, {}
 
         def load(g):
             emb_sb[g] = emb_pool.tile([P, GROUP, FEAT], BF16, name="emb_sb")
@@ -98,14 +99,18 @@ def tile_densegatlayer_pb_kernel(
         e_mask = consts.tile([P, NODES], F32, name="e_mask")
         nc.vector.tensor_scalar_mul(out=e_mask[:], in0=mask_row[:], scalar1=mask_col[:, 0:1])
 
+        def in_range(g):
+            return 0 <= g < N_GROUPS
+
         def handed_over(g, k):
             return k in (SCALED, SHAPED) and g < N_GROUPS - 1
 
-        def mask(g):
-            xe_bf[g] = front.tile([P, GROUP, FEAT], BF16, name="xe_bf")
-            for k in range(GROUP):
+        def mask(g, tiles, by_scalar):
+            if g not in xe_bf:
+                xe_bf[g] = xe_pool.tile([P, GROUP, FEAT], BF16, name="xe_bf")
+            for k in tiles:
                 j = g * GROUP + k
-                if g < HEAD_MASKS:
+                if by_scalar:
                     nc.scalar.activation(
                         out=xe_bf[g][:, k, :], in_=emb_sb[g][:, k, :], func=ACT.Copy, scale=e_mask[:, j : j + 1]
                     )
@@ -113,6 +118,12 @@ def tile_densegatlayer_pb_kernel(
                     nc.vector.tensor_scalar_mul(
                         out=xe_bf[g][:, k, :], in0=emb_sb[g][:, k, :], scalar1=e_mask[:, j : j + 1]
                     )
+
+        def tiles_of_scalar(g):
+            return range(GROUP - 1, GROUP) if g >= SCALAR_MASKS_FROM else ()
+
+        def tiles_of_vector(g):
+            return [k for k in range(GROUP) if k not in tiles_of_scalar(g)]
 
         def transpose(g):
             xt[g] = []
@@ -246,7 +257,7 @@ def tile_densegatlayer_pb_kernel(
             nc.gpsimd.tensor_scalar(
                 out=res[g][:, SHAPED, :],
                 in0=y[g][:, SHAPED, :],
-                scalar1=neg_mean[g][:, SHAPED : SHAPED + 1],
+                scalar1=turn[g],
                 scalar2=rstd[g][:, SHAPED : SHAPED + 1],
                 op0=ALU.add,
                 op1=ALU.mult,
@@ -268,8 +279,11 @@ def tile_densegatlayer_pb_kernel(
             )
 
         def take_turn(g):
-            turn = small.tile([P, 1], U32, name="turn")
-            nc.gpsimd.tensor_copy(out=turn[:], in_=codes[g][:, 0:1])
+            turn[g] = neg_mean[g][:, SHAPED : SHAPED + 1]
+            if in_range(g + 4):
+                copied = small.tile([P, 1], F32, name="copied")
+                nc.vector.tensor_copy(out=copied[:], in_=turn[g])
+                turn[g] = copied[:]
 
         w_codes = consts.tile([P, 3, FEAT], U32, name="w_codes", align_bytes=64)
         w_scales = consts.tile([P, 3, FEAT], U8, name="w_scales", align_bytes=64)
@@ -318,7 +332,7 @@ def tile_densegatlayer_pb_kernel(
         node_t = psum_t.tile([P, PAIR, HALVES, P], F32, name="xt")
         for u in range(HALVES):
             nc.tensor.transpose(node_t[:, 0, u, :], node_sb[:].bitcast(F32)[:, u * P : (u + 1) * P], ident[:])
-        mask(0)
+        mask(0, range(GROUP), by_scalar=True)
         transpose(0)
         for h in range(GROUP // PAIR):
             unload(0, h)
@@ -348,7 +362,7 @@ def tile_densegatlayer_pb_kernel(
                 in_=node_scales[:].rearrange("p (b j) -> p b j", b=GRAPHS),
             )
         quantise(0)
-        mask(1)
+        mask(1, range(GROUP), by_scalar=False)
         transpose(1)
         for h in range(GROUP // PAIR):
             unload(1, h)
@@ -365,8 +379,9 @@ def tile_densegatlayer_pb_kernel(
             products(0, f)
         repeat_nodes(1, 2)
         quantise(1)
-        mask(2)
+        mask(2, range(GROUP), by_scalar=False)
         turn_back(0, 0)
+        turn_back(0, 1)
         transpose(2)
         gamma_beta_ps = psum_const.tile([P, 2, FEAT], BF16, name="gamma_beta_ps")
         for v in range(2):
@@ -377,9 +392,6 @@ def tile_densegatlayer_pb_kernel(
         nc.scalar.copy(out=beta_sb[:], in_=gamma_beta_ps[:, 1, :])
         repeat_nodes(2, 7)
 
-        def in_range(g):
-            return 0 <= g < N_GROUPS
-
         for i in range(N_GROUPS + 2):
             if in_range(i + LOADS_AHEAD):
                 load(i + LOADS_AHEAD)
@@ -388,14 +400,16 @@ def tile_densegatlayer_pb_kernel(
             if in_range(i - 2):
                 finish_statistics(i - 2)
             for k in range(GROUP):
-                if in_range(i):
-                    if k + 1 < GROUP:
-                        turn_back(i, k + 1)
-                    residual(i, k)
                 if in_range(i + 2) and k < GROUP // PAIR:
                     unload(i + 2, k)
-                if in_range(i + 1):
-                    products(i + 1, k)
+                if k % PAIR == 0:
+                    if in_range(i + 1):
+                        for f in range(k, k + PAIR):
+                            products(i + 1, f)
+                    if in_range(i):
+                        turn_back(i, PAIR + k // PAIR)
+                if in_range(i):
+                    residual(i, k)
                 if in_range(i - 1):
                     centre_and_gain(i - 1, k)
                     deviation(i - 1, k)
@@ -405,16 +419,19 @@ def tile_densegatlayer_pb_kernel(
                     repeat_nodes(7 + 3 * k, min(10 + 3 * k, N_GROUPS))
                 if k == 1:
                     if in_range(i + 3):
-                        mask(i + 3)
+                        mask(i + 3, tiles_of_vector(i + 3), by_scalar=False)
                     if in_range(i + 2):
                         quantise(i + 2)
+                    if in_range(i - 2) and i - 2 < N_GROUPS - 1:
+                        take_turn(i - 2)
+            if in_range(i + 4):
+                mask(i + 4, tiles_of_scalar(i + 4), by_scalar=True)
             if in_range(i + 3):
                 transpose(i + 3)
             if in_range(i + 1):
-                turn_back(i + 1, 0)
+                for k in range(PAIR):
+                    turn_back(i + 1, k)
             if in_range(i - 3) and i - 3 < N_GROUPS - 1:
                 store(i - 3, SCALED, 2)
             if in_range(i - 2) and i - 2 < N_GROUPS - 1:
-                if in_range(i + 2):
-                    take_turn(i + 2)
                 normalise_handed_over(i - 2)

@@ -59,6 +59,16 @@ def tile_densegatlayer_pb_kernel(
             emb_sb[g] = emb_pool.tile([P, GROUP, FEAT], BF16, name="emb_sb")
             nc.sync.dma_start(out=emb_sb[g][:], in_=emb_rows[:, g * GROUP : (g + 1) * GROUP, :])
 
+        w_raw = {}
+
+        def load_w(blk):
+            w_raw[blk] = w_stage.tile([P, PACK, FEAT], BF16, name="w_raw")
+            nc.sync.dma_start(
+                out=w_raw[blk][:].rearrange("p (u e) n -> p u (e n)", u=HALVES),
+                in_=Wedge[blk * FEAT : (blk + 1) * FEAT, :].rearrange("(u p e) n -> p u (e n)", u=HALVES, p=P),
+            )
+
+        load_w(2)
         mask_col_bf = consts.tile([P, 1], BF16, name="mask_col_bf")
         nc.sync.dma_start(out=mask_col_bf[:], in_=node_mask.rearrange("b (n o) -> (b n) o", o=1))
         mask_row = consts.tile([P, NODES], BF16, name="mask_row")
@@ -69,15 +79,9 @@ def tile_densegatlayer_pb_kernel(
             )
         node_sb = consts.tile([P, FEAT], BF16, name="node_sb")
         nc.sync.dma_start(out=node_sb[:], in_=new_node.rearrange("b n f -> (b n) f"))
-        w_raw = {}
-        for blk in (2, 1, 0):
-            w_raw[blk] = w_stage.tile([P, PACK, FEAT], BF16, name="w_raw")
-            nc.sync.dma_start(
-                out=w_raw[blk][:].rearrange("p (u e) n -> p u (e n)", u=HALVES),
-                in_=Wedge[blk * FEAT : (blk + 1) * FEAT, :].rearrange("(u p e) n -> p u (e n)", u=HALVES, p=P),
-            )
-            if blk == 2:
-                load(0)
+        load(0)
+        load_w(1)
+        load_w(0)
         vec_rows = consts.tile([P, 3, FEAT], BF16, name="vec_rows")
         nc.vector.memset(vec_rows[:], 0.0)
         for v, vec in enumerate((gamma_e, beta_e, bedge)):
@@ -103,7 +107,10 @@ def tile_densegatlayer_pb_kernel(
             return 0 <= g < N_GROUPS
 
         def handed_over(g, k):
-            return k in (SCALED, SHAPED) and g < N_GROUPS - 1
+            return (k == SHAPED and g < N_GROUPS - 1) or (k == SCALED and g < N_GROUPS - 2)
+
+        def first_handed_over(g):
+            return SCALED if handed_over(g, SCALED) else SHAPED
 
         def mask(g, tiles, by_scalar):
             if g not in xe_bf:
@@ -262,20 +269,25 @@ def tile_densegatlayer_pb_kernel(
                 op0=ALU.add,
                 op1=ALU.mult,
             )
-            nc.gpsimd.tensor_scalar(
-                out=res[g][:, SCALED, :],
-                in0=res[g][:, SCALED, :],
-                scalar1=rstd[g][:, SCALED : SCALED + 1],
-                scalar2=0.0,
-                op0=ALU.mult,
-                op1=ALU.add,
-            )
+            if handed_over(g, SCALED):
+                nc.gpsimd.tensor_scalar(
+                    out=res[g][:, SCALED, :],
+                    in0=res[g][:, SCALED, :],
+                    scalar1=rstd[g][:, SCALED : SCALED + 1],
+                    scalar2=0.0,
+                    op0=ALU.mult,
+                    op1=ALU.add,
+                )
             nc.gpsimd.tensor_tensor(
                 out=res[g][:, SHAPED, :], in0=res[g][:, SHAPED, :], in1=gamma_sb[:], op=ALU.mult
             )
-            both = res[g][:, SCALED : SHAPED + 1, :]
+            first = first_handed_over(g)
+            tiles = res[g][:, first : SHAPED + 1, :]
             nc.gpsimd.tensor_tensor(
-                out=both, in0=both, in1=beta_sb[:].unsqueeze(1).to_broadcast([P, 2, FEAT]), op=ALU.add
+                out=tiles,
+                in0=tiles,
+                in1=beta_sb[:].unsqueeze(1).to_broadcast([P, SHAPED + 1 - first, FEAT]),
+                op=ALU.add,
             )
 
         def take_turn(g):
@@ -361,8 +373,8 @@ def tile_densegatlayer_pb_kernel(
                 out=scales4[:].rearrange("p (j b) r -> p b j r", b=GRAPHS)[:, :, :, r],
                 in_=node_scales[:].rearrange("p (b j) -> p b j", b=GRAPHS),
             )
-        quantise(0)
         mask(1, range(GROUP), by_scalar=False)
+        quantise(0)
         transpose(1)
         for h in range(GROUP // PAIR):
             unload(1, h)
@@ -387,18 +399,16 @@ def tile_densegatlayer_pb_kernel(
         for v in range(2):
             nc.tensor.matmul(out=gamma_beta_ps[:, v, :], lhsT=ones[:], rhs=vec_rows[:, v, :], start=True, stop=True)
         gamma_sb = consts.tile([P, FEAT], F32, name="gamma_sb")
-        nc.scalar.copy(out=gamma_sb[:], in_=gamma_beta_ps[:, 0, :])
         beta_sb = consts.tile([P, FEAT], F32, name="beta_sb")
-        nc.scalar.copy(out=beta_sb[:], in_=gamma_beta_ps[:, 1, :])
-        repeat_nodes(2, 7)
+        repeat_nodes(2, 10)
 
         for i in range(N_GROUPS + 2):
             if in_range(i + LOADS_AHEAD):
                 load(i + LOADS_AHEAD)
-            if in_range(i - 1):
-                mean(i - 1)
             if in_range(i - 2):
                 finish_statistics(i - 2)
+            if in_range(i - 1):
+                mean(i - 1)
             for k in range(GROUP):
                 if in_range(i + 2) and k < GROUP // PAIR:
                     unload(i + 2, k)
@@ -410,13 +420,13 @@ def tile_densegatlayer_pb_kernel(
                         turn_back(i, PAIR + k // PAIR)
                 if in_range(i):
                     residual(i, k)
+                if in_range(i - 2):
+                    normalise(i - 2, k)
                 if in_range(i - 1):
                     centre_and_gain(i - 1, k)
                     deviation(i - 1, k)
-                if in_range(i - 2):
-                    normalise(i - 2, k)
                 if i == 0 and k < 3:
-                    repeat_nodes(7 + 3 * k, min(10 + 3 * k, N_GROUPS))
+                    repeat_nodes(10 + 2 * k, 12 + 2 * k)
                 if k == 1:
                     if in_range(i + 3):
                         mask(i + 3, tiles_of_vector(i + 3), by_scalar=False)
@@ -424,6 +434,9 @@ def tile_densegatlayer_pb_kernel(
                         quantise(i + 2)
                     if in_range(i - 2) and i - 2 < N_GROUPS - 1:
                         take_turn(i - 2)
+            if i == 0:
+                nc.scalar.copy(out=gamma_sb[:], in_=gamma_beta_ps[:, 0, :])
+                nc.scalar.copy(out=beta_sb[:], in_=gamma_beta_ps[:, 1, :])
             if in_range(i + 4):
                 mask(i + 4, tiles_of_scalar(i + 4), by_scalar=True)
             if in_range(i + 3):
@@ -432,6 +445,7 @@ def tile_densegatlayer_pb_kernel(
                 for k in range(PAIR):
                     turn_back(i + 1, k)
             if in_range(i - 3) and i - 3 < N_GROUPS - 1:
-                store(i - 3, SCALED, 2)
+                first = first_handed_over(i - 3)
+                store(i - 3, first, SHAPED + 1 - first)
             if in_range(i - 2) and i - 2 < N_GROUPS - 1:
                 normalise_handed_over(i - 2)

import concourse.mybir as mybir
from concourse.masks import make_identity

BF16 = mybir.dt.bfloat16
F32 = mybir.dt.float32
I32 = mybir.dt.int32
U32 = mybir.dt.uint32
U8 = mybir.dt.uint8
FP8X4 = mybir.dt.float8_e4m3fn_x4
ALU = mybir.AluOpType
ACT = mybir.ActivationFunctionType

P = 128
PACK = 4
HALVES = 2
GRAPHS = 2
NODES = 64
FEAT = 512
BLOCKS = FEAT // P
GROUP = 4
N_GROUPS = NODES // GROUP
PAIR = 2
REP = 4
LOADS_AHEAD = 5
SCALAR_MASKS_FROM = 4
SCALED = 2
SHAPED = 3
LN_EPS = 1e-5

FLOPS = 2 * (GRAPHS * NODES * NODES + 2 * GRAPHS * NODES) * FEAT * FEAT


def tile_densegatlayer_pb_kernel(
    tc, new_node, emb_edge, node_mask, Wedge, bedge, gamma_e, beta_e, out
):
    nc = tc.nc
    emb_rows = emb_edge.rearrange("b i j f -> (b i) j f")
    out_rows = out.rearrange("b i j f -> (b i) j f")

    with (
        tc.tile_pool(name="consts", bufs=1) as consts,
        tc.tile_pool(name="w_stage", bufs=3) as w_stage,
        tc.tile_pool(name="emb_pool", bufs=LOADS_AHEAD + 2) as emb_pool,
        tc.tile_pool(name="xe_pool", bufs=3) as xe_pool,
        tc.tile_pool(name="front", bufs=2) as front,
        tc.tile_pool(name="y_pool", bufs=4) as y_pool,
        tc.tile_pool(name="back", bufs=4) as back,
        tc.tile_pool(name="small", bufs=4) as small,
        tc.psum_pool(name="psum_const", bufs=1) as psum_const,
        tc.psum_pool(name="psum_t", bufs=2) as psum_t,
        tc.psum_pool(name="psum_prod", bufs=2) as psum_prod,
        tc.psum_pool(name="psum_acc", bufs=3) as psum_acc,
        tc.manual_schedule(),
    ):
        emb_sb, xe_bf, xt, grouped, codes, scales, prod_t = {}, {}, {}, {}, {}, {}, {}
        acc, y, row_sum, neg_mean, turn, sq_sum, rstd, res = {}, {}, {}, {}, {}, {}, {}, {}

        def load(g):
            emb_sb[g] = emb_pool.tile([P, GROUP, FEAT], BF16, name="emb_sb")
            nc.sync.dma_start(out=emb_sb[g][:], in_=emb_rows[:, g * GROUP : (g + 1) * GROUP, :])

        w_raw = {}

        def load_w(blk):
            w_raw[blk] = w_stage.tile([P, PACK, FEAT], BF16, name="w_raw")
            nc.sync.dma_start(
                out=w_raw[blk][:].rearrange("p (u e) n -> p u (e n)", u=HALVES),
                in_=Wedge[blk * FEAT : (blk + 1) * FEAT, :].rearrange("(u p e) n -> p u (e n)", u=HALVES, p=P),
            )

        load_w(2)
        mask_col_bf = consts.tile([P, 1], BF16, name="mask_col_bf")
        nc.sync.dma_start(out=mask_col_bf[:], in_=node_mask.rearrange("b (n o) -> (b n) o", o=1))
        mask_row = consts.tile([P, NODES], BF16, name="mask_row")
        for b in range(GRAPHS):
            nc.sync.dma_start(
                out=mask_row[b * NODES : (b + 1) * NODES, :],
                in_=node_mask[b : b + 1, :].rearrange("o n -> (o n)").partition_broadcast(NODES),
            )
        node_sb = consts.tile([P, FEAT], BF16, name="node_sb")
        nc.sync.dma_start(out=node_sb[:], in_=new_node.rearrange("b n f -> (b n) f"))
        load(0)
        load_w(1)
        load_w(0)
        vec_rows = consts.tile([P, 3, FEAT], BF16, name="vec_rows")
        nc.vector.memset(vec_rows[:], 0.0)
        for v, vec in enumerate((gamma_e, beta_e, bedge)):
            nc.sync.dma_start(out=vec_rows[0:1, v, :], in_=vec.rearrange("(o f) -> o f", o=1))
        for g in range(1, LOADS_AHEAD):
            load(g)

        ident = consts.tile([P, P], F32, name="ident")
        make_identity(nc, ident[:])
        ones = consts.tile([P, P], BF16, name="ones")
        nc.vector.memset(ones[:], 1.0)
        eps = consts.tile([P, 1], F32, name="eps")
        nc.vector.memset(eps[:], LN_EPS)
        warm = consts.tile([P, 1], F32, name="warm")
        nc.scalar.activation(out=warm[:], in_=eps[:], func=ACT.Abs_reciprocal_sqrt)

        mask_col = consts.tile([P, 1], F32, name="mask_col")
        nc.vector.tensor_copy(out=mask_col[:], in_=mask_col_bf[:])
        e_mask = consts.tile([P, NODES], F32, name="e_mask")
        nc.vector.tensor_scalar_mul(out=e_mask[:], in0=mask_row[:], scalar1=mask_col[:, 0:1])

        def in_range(g):
            return 0 <= g < N_GROUPS

        def handed_over(g, k):
            return (k == SHAPED and g < N_GROUPS - 1) or (k == SCALED and g < N_GROUPS - 2)

        def first_handed_over(g):
            return SCALED if handed_over(g, SCALED) else SHAPED

        def mask(g, tiles, by_scalar):
            if g not in xe_bf:
                xe_bf[g] = xe_pool.tile([P, GROUP, FEAT], BF16, name="xe_bf")
            for k in tiles:
                j = g * GROUP + k
                if by_scalar:
                    nc.scalar.activation(
                        out=xe_bf[g][:, k, :], in_=emb_sb[g][:, k, :], func=ACT.Copy, scale=e_mask[:, j : j + 1]
                    )
                else:
                    nc.vector.tensor_scalar_mul(
                        out=xe_bf[g][:, k, :], in0=emb_sb[g][:, k, :], scalar1=e_mask[:, j : j + 1]
                    )

        def tiles_of_scalar(g):
            return range(GROUP - 1, GROUP) if g >= SCALAR_MASKS_FROM else ()

        def tiles_of_vector(g):
            return [k for k in range(GROUP) if k not in tiles_of_scalar(g)]

        def transpose(g):
            xt[g] = []
            for h in range(GROUP // PAIR):
                bank = psum_t.tile([P, PAIR, HALVES, P], F32, name="xt")
                for k in range(PAIR):
                    words = xe_bf[g][:, h * PAIR + k, :].bitcast(F32)
                    for u in range(HALVES):
                        nc.tensor.transpose(bank[:, k, u, :], words[:, u * P : (u + 1) * P], ident[:])
                xt[g].append(bank)

        def unload(g, h):
            if h == 0:
                grouped[g] = front.tile([P, GROUP, P, PACK], BF16, name="grouped", align_bytes=64)
            nc.scalar.copy(
                out=grouped[g][:, h * PAIR : (h + 1) * PAIR, :, :].bitcast(F32),
                in_=xt[g][h][:].rearrange("p k u r -> p k r u"),
            )

        def quantise(g):
            codes[g] = front.tile([P, GROUP * P], U32, name="codes", align_bytes=64)
            scales[g] = front.tile([P, GROUP * P], U8, name="scales", align_bytes=64)
            nc.vector.quantize_mx(
                out=codes[g][:].bitcast(FP8X4),
                scales=scales[g][:],
                in_=grouped[g][:].rearrange("p k r t -> p (k r t)"),
            )

        def products(g, f):
            features = slice(f * P, (f + 1) * P)
            rows = slice(g * GROUP * P, (g + 1) * GROUP * P)
            bank = psum_prod.tile([P, GROUP * P], F32, name="prod")
            operands = (
                (2, codes[g][:], scales[g][:]),
                (1, col_codes[:, rows], col_scales[:, rows]),
                (0, row_codes[:], row_scales[:]),
            )
            for n, (blk, row_words, row_bytes) in enumerate(operands):
                nc.tensor.matmul_mx(
                    out=bank[:],
                    lhsT=w_codes[:, blk, features].bitcast(FP8X4),
                    lhsT_scale=w_scales[:, blk, features],
                    rhs=row_words.bitcast(FP8X4),
                    rhs_scale=row_bytes,
                    start=n == 0,
                    stop=n == len(operands) - 1,
                )
            if f == 0:
                prod_t[g] = front.tile([P, BLOCKS, GROUP, P], F32, name="prod_t")
            nc.scalar.activation(
                out=prod_t[g][:, f, :, :].rearrange("p k r -> p (k r)"),
                in_=bank[:],
                func=ACT.Identity,
                bias=bias_col[:, f : f + 1],
                scale=1.0,
            )

        def turn_back(g, k):
            acc[g, k] = psum_acc.tile([P, FEAT], F32, name="acc")
            for f in range(BLOCKS):
                nc.tensor.transpose(acc[g, k][:, f * P : (f + 1) * P], prod_t[g][:, f, k, :], ident[:])

        def residual(g, k):
            if k == 0:
                y[g] = y_pool.tile([P, GROUP, FEAT], F32, name="y")
                row_sum[g] = small.tile([P, GROUP], F32, name="row_sum")
            j = g * GROUP + k
            nc.vector.scalar_tensor_tensor(
                out=y[g][:, k, :],
                in0=emb_sb[g][:, k, :],
                scalar=e_mask[:, j : j + 1],
                in1=acc[g, k][:],
                op0=ALU.mult,
                op1=ALU.add,
                accum_out=row_sum[g][:, k : k + 1],
            )

        def mean(g):
            neg_mean[g] = small.tile([P, GROUP], F32, name="neg_mean")
            nc.scalar.activation(out=neg_mean[g][:], in_=row_sum[g][:], func=ACT.Copy, scale=-1.0 / FEAT)

        def deviation(g, k):
            if k == 0:
                sq_sum[g] = small.tile([P, GROUP], F32, name="sq_sum")
            squares = small.tile([P, FEAT], BF16, name="squares")
            nc.scalar.activation(
                out=squares[:],
                in_=y[g][:, k, :],
                func=ACT.Square,
                bias=neg_mean[g][:, k : k + 1],
                scale=1.0,
                accum_out=sq_sum[g][:, k : k + 1],
            )

        def finish_statistics(g):
            rstd[g] = small.tile([P, GROUP], F32, name="rstd")
            nc.scalar.activation(
                out=rstd[g][:], in_=sq_sum[g][:], func=ACT.Abs_reciprocal_sqrt, bias=eps[:, 0:1], scale=1.0 / FEAT
            )

        def centre_and_gain(g, k):
            if k == 0:
                res[g] = back.tile([P, GROUP, FEAT], F32, name="res")
            if not (handed_over(g, k) and k == SHAPED):
                nc.vector.scalar_tensor_tensor(
                    out=res[g][:, k, :],
                    in0=y[g][:, k, :],
                    scalar=neg_mean[g][:, k : k + 1],
                    in1=gamma_beta_ps[:, 0, :],
                    op0=ALU.add,
                    op1=ALU.mult,
                )

        def store(g, k, n=1):
            j = g * GROUP + k
            nc.sync.dma_start(out=out_rows[:, j : j + n, :], in_=res[g][:, k : k + n, :])

        def normalise(g, k):
            if not handed_over(g, k):
                nc.vector.scalar_tensor_tensor(
                    out=res[g][:, k, :],
                    in0=res[g][:, k, :],
                    scalar=rstd[g][:, k : k + 1],
                    in1=gamma_beta_ps[:, 1, :],
                    op0=ALU.mult,
                    op1=ALU.add,
                )
                store(g, k)

        def normalise_handed_over(g):
            nc.gpsimd.tensor_scalar(
                out=res[g][:, SHAPED, :],
                in0=y[g][:, SHAPED, :],
                scalar1=turn[g],
                scalar2=rstd[g][:, SHAPED : SHAPED + 1],
                op0=ALU.add,
                op1=ALU.mult,
            )
            if handed_over(g, SCALED):
                nc.gpsimd.tensor_scalar(
                    out=res[g][:, SCALED, :],
                    in0=res[g][:, SCALED, :],
                    scalar1=rstd[g][:, SCALED : SCALED + 1],
                    scalar2=0.0,
                    op0=ALU.mult,
                    op1=ALU.add,
                )
            nc.gpsimd.tensor_tensor(
                out=res[g][:, SHAPED, :], in0=res[g][:, SHAPED, :], in1=gamma_sb[:], op=ALU.mult
            )
            first = first_handed_over(g)
            tiles = res[g][:, first : SHAPED + 1, :]
            nc.gpsimd.tensor_tensor(
                out=tiles,
                in0=tiles,
                in1=beta_sb[:].unsqueeze(1).to_broadcast([P, SHAPED + 1 - first, FEAT]),
                op=ALU.add,
            )

        def take_turn(g):
            turn[g] = neg_mean[g][:, SHAPED : SHAPED + 1]
            if in_range(g + 4):
                copied = small.tile([P, 1], F32, name="copied")
                nc.vector.tensor_copy(out=copied[:], in_=turn[g])
                turn[g] = copied[:]

        w_codes = consts.tile([P, 3, FEAT], U32, name="w_codes", align_bytes=64)
        w_scales = consts.tile([P, 3, FEAT], U8, name="w_scales", align_bytes=64)
        w_grouped = {}

        def regroup_w(blk, copy):
            w_grouped[blk] = w_stage.tile([P, FEAT, PACK], BF16, name="w_grouped", align_bytes=64)
            copy(
                out=w_grouped[blk][:].rearrange("p (n i) t -> p n t i", i=4),
                in_=w_raw[blk][:].rearrange("p t (n i) -> p n t i", i=4),
            )

        def quantise_w(blk):
            nc.vector.quantize_mx(
                out=w_codes[:, blk, :].bitcast(FP8X4),
                scales=w_scales[:, blk, :],
                in_=w_grouped[blk][:].rearrange("p n t -> p (n t)"),
            )

        node_codes = consts.tile([P, P], U32, name="node_codes", align_bytes=64)
        node_scales = consts.tile([P, P], U8, name="node_scales", align_bytes=64)
        nc.vector.memset(node_scales[:].bitcast(I32), 0)
        scales4 = consts.tile([P, NODES * GRAPHS, REP], U8, name="scales4", align_bytes=64)
        col_codes = consts.tile([P, NODES * P], U32, name="col_codes", align_bytes=64)
        col_scales = consts.tile([P, NODES * P], U8, name="col_scales", align_bytes=64)
        row_codes = consts.tile([P, GROUP * P], U32, name="row_codes", align_bytes=64)
        row_scales = consts.tile([P, GROUP * P], U8, name="row_scales", align_bytes=64)

        def repeat_nodes(g0, g1):
            j0, j1 = g0 * GROUP, g1 * GROUP
            nc.vector.tensor_copy(
                out=col_scales[:, j0 * P : j1 * P].bitcast(I32).rearrange("p (a s) -> p a s", a=(j1 - j0) * GRAPHS),
                in_=scales4[:, j0 * GRAPHS : j1 * GRAPHS, :]
                .bitcast(I32)
                .to_broadcast([P, (j1 - j0) * GRAPHS, NODES // REP]),
            )
            nc.vector.tensor_copy(
                out=col_codes[:, j0 * P : j1 * P].bitcast(I32).rearrange("p (j b s) -> p j b s", b=GRAPHS, s=NODES),
                in_=node_codes[:]
                .bitcast(I32)
                .rearrange("p (b j) -> p j b", b=GRAPHS)[:, j0:j1, :]
                .unsqueeze(3)
                .to_broadcast([P, j1 - j0, GRAPHS, NODES]),
            )

        node_t = psum_t.tile([P, PAIR, HALVES, P], F32, name="xt")
        for u in range(HALVES):
            nc.tensor.transpose(node_t[:, 0, u, :], node_sb[:].bitcast(F32)[:, u * P : (u + 1) * P], ident[:])
        mask(0, range(GROUP), by_scalar=True)
        transpose(0)
        for h in range(GROUP // PAIR):
            unload(0, h)
        regroup_w(0, nc.scalar.copy)
        bias_ps = psum_acc.tile([P, BLOCKS, 2], F32, name="acc")
        for f in range(BLOCKS):
            nc.tensor.matmul(
                out=bias_ps[:, f, :], lhsT=vec_rows[:, 2, f * P : (f + 1) * P], rhs=ones[:, 0:2], start=True, stop=True
            )
        bias_col = consts.tile([P, BLOCKS], F32, name="bias_col")
        nc.scalar.copy(out=bias_col[:], in_=bias_ps[:, :, 0])
        regroup_w(2, nc.vector.tensor_copy)
        node_grouped = consts.tile([P, GRAPHS, NODES, PACK], BF16, name="node_grouped", align_bytes=64)
        nc.vector.tensor_copy(
            out=node_grouped[:].bitcast(F32), in_=node_t[:, 0, :, :].rearrange("p u (b n) -> p b n u", b=GRAPHS)
        )
        quantise_w(2)
        nc.vector.quantize_mx(
            out=node_codes[:].bitcast(FP8X4),
            scales=node_scales[:],
            in_=node_grouped[:].rearrange("p b n t -> p (b n t)"),
        )
        regroup_w(1, nc.vector.tensor_copy)
        for r in range(REP):
            nc.vector.tensor_copy(
                out=scales4[:].rearrange("p (j b) r -> p b j r", b=GRAPHS)[:, :, :, r],
                in_=node_scales[:].rearrange("p (b j) -> p b j", b=GRAPHS),
            )
        mask(1, range(GROUP), by_scalar=False)
        quantise(0)
        transpose(1)
        for h in range(GROUP // PAIR):
            unload(1, h)
        quantise_w(1)
        repeat_nodes(0, 1)
        for out_tile, in_tile in ((row_codes, node_codes), (row_scales, node_scales)):
            words = in_tile[:].bitcast(I32)
            nc.vector.tensor_copy(
                out=out_tile[:].bitcast(I32).rearrange("p (k r) -> p k r", k=GROUP),
                in_=words.unsqueeze(1).to_broadcast([P, GROUP, words.shape[1]]),
            )
        quantise_w(0)
        for f in range(BLOCKS):
            products(0, f)
        repeat_nodes(1, 2)
        quantise(1)
        mask(2, range(GROUP), by_scalar=False)
        turn_back(0, 0)
        turn_back(0, 1)
        transpose(2)
        gamma_beta_ps = psum_const.tile([P, 2, FEAT], BF16, name="gamma_beta_ps")
        for v in range(2):
            nc.tensor.matmul(out=gamma_beta_ps[:, v, :], lhsT=ones[:], rhs=vec_rows[:, v, :], start=True, stop=True)
        gamma_sb = consts.tile([P, FEAT], F32, name="gamma_sb")
        beta_sb = consts.tile([P, FEAT], F32, name="beta_sb")
        repeat_nodes(2, 10)

        for i in range(N_GROUPS + 2):
            if in_range(i + LOADS_AHEAD):
                load(i + LOADS_AHEAD)
            if in_range(i - 2):
                finish_statistics(i - 2)
            if in_range(i - 1):
                mean(i - 1)
            for k in range(GROUP):
                if in_range(i + 2) and k < GROUP // PAIR:
                    unload(i + 2, k)
                if k % PAIR == 0:
                    if in_range(i + 1):
                        for f in range(k, k + PAIR):
                            products(i + 1, f)
                    if in_range(i):
                        turn_back(i, PAIR + k // PAIR)
                if in_range(i):
                    residual(i, k)
                if in_range(i - 2):
                    normalise(i - 2, k)
                if in_range(i - 1):
                    centre_and_gain(i - 1, k)
                    deviation(i - 1, k)
                if i == 0 and k < 3:
                    repeat_nodes(10 + 2 * k, 12 + 2 * k)
                if k == 1:
                    if in_range(i + 3):
                        mask(i + 3, tiles_of_vector(i + 3), by_scalar=False)
                    if in_range(i + 2):
                        quantise(i + 2)
                    if in_range(i - 2) and i - 2 < N_GROUPS - 1:
                        take_turn(i - 2)
            if i == 0:
                nc.scalar.copy(out=gamma_sb[:], in_=gamma_beta_ps[:, 0, :])
                nc.scalar.copy(out=beta_sb[:], in_=gamma_beta_ps[:, 1, :])
            if in_range(i + 4):
                mask(i + 4, tiles_of_scalar(i + 4), by_scalar=True)
            if in_range(i + 3):
                transpose(i + 3)
            if in_range(i + 1):
                for k in range(PAIR):
                    turn_back(i + 1, k)
            if in_range(i - 3) and i - 3 < N_GROUPS - 1:
                first = first_handed_over(i - 3)
                store(i - 3, first, SHAPED + 1 - first)
            if in_range(i - 2) and i - 2 < N_GROUPS - 1:
                normalise_handed_over(i - 2)
